import numpy as np
import ml_dtypes

BF16 = ml_dtypes.bfloat16


def bf(x):
    return np.asarray(x, np.float32).astype(BF16)


def f32(x):
    return np.asarray(x, np.float32)


def f64(x):
    return np.asarray(x).astype(np.float64)


def striped(idx):
    return np.tile(idx.reshape(-1, 16).T, (8, 1))


E, NH, NKV, D, C, S, L, B, WIN, N = 512, 4, 2, 128, 256, 1024, 512, 4, 128, 2048
NEG = -1e30


def rot(a):
    return np.concatenate([-a[D // 2:], a[:D // 2]], axis=0)


def setup_inputs():
    ang = 2.0 * np.pi * np.random.random_sample((D // 2, S))
    return {"x": bf(np.random.standard_normal((E, N))), "wq": bf(np.random.standard_normal((E, NH * D)) / np.sqrt(E)), "wk": bf(np.random.standard_normal((E, NKV * D)) / np.sqrt(E)), "wv": bf(2.0 * np.random.standard_normal((E, NKV * D)) / np.sqrt(E)), "wo": bf(2.0 * np.random.standard_normal((NH * D, E)) / np.sqrt(NH * D)), "rope": f32(np.concatenate([np.cos(ang), np.cos(ang), np.sin(ang), np.sin(ang)], axis=0)), "offs": striped(np.concatenate([np.random.permutation(S)[:L] for _ in range(B)]))}


def reference(x, wq, wk, wv, wo, rope, offs):
    idx = offs[:16].T.reshape(-1)
    xs = f64(x)
    r = f64(rope)[:, idx]
    cs = r[:D]
    sn = r[D:C]
    i = np.arange(L)
    keep = (i[:, None] <= i[None, :]) & (i[None, :] - i[:, None] <= WIN)
    kr = []
    vp = []
    for u in range(NKV):
        kp = f64(wk)[:, u * D:(u + 1) * D].T @ xs
        kr.append(cs * kp + sn * rot(kp))
        vp.append(f64(wv)[:, u * D:(u + 1) * D].T @ xs)
    att = np.zeros((NH * D, N))
    for h in range(NH):
        qp = f64(wq)[:, h * D:(h + 1) * D].T @ xs
        qr = cs * qp + sn * rot(qp)
        u = h // (NH // NKV)
        for b in range(B):
            sl = slice(b * L, (b + 1) * L)
            sc = kr[u][:, sl].T @ qr[:, sl] / np.sqrt(D)
            sc = np.where(keep, sc, NEG)
            w = np.exp(sc - sc.max(axis=0, keepdims=True))
            w = w / w.sum(axis=0, keepdims=True)
            att[h * D:(h + 1) * D, sl] = vp[u][:, sl] @ w
    return f64(wo).T @ att

@@ -1,0 +1,193 @@
+import math
+
+import concourse.mybir as mybir
+from concourse.masks import make_identity
+
+BF16, F32, U16 = mybir.dt.bfloat16, mybir.dt.float32, mybir.dt.uint16
+ADD, MULT, MAX, IS_GE = (
+    mybir.AluOpType.add,
+    mybir.AluOpType.mult,
+    mybir.AluOpType.max,
+    mybir.AluOpType.is_ge,
+)
+EXP, COPY = mybir.ActivationFunctionType.Exp, mybir.ActivationFunctionType.Copy
+X_AXIS = mybir.AxisListType.X
+
+P = 128
+E = 512
+N = 2048
+HEADS, KV_HEADS = 4, 2
+GROUP = HEADS // KV_HEADS
+SEQ = 512
+N_SEQ = N // SEQ
+POSITIONS = 1024
+E_BLOCKS = E // P
+BLOCKS = SEQ // P
+HALF = P // 2
+MASKED = -1e30
+
+SEEN_PAIRS = N_SEQ * (P * (P + 1) // 2 + (SEQ - P) * (P + 1))
+FLOPS = 2 * N * E * (HEADS + 2 * KV_HEADS) * P + 2 * N * HEADS * P * E + 4 * HEADS * P * SEEN_PAIRS
+
+
+def tile_unpaddedmistralattention_b_kernel(tc, x, wq, wk, wv, wo, rope, offs, out):
+    nc = tc.nc
+    with (
+        tc.tile_pool(name="held", bufs=1) as held,
+        tc.tile_pool(name="work", bufs=3) as work,
+        tc.tile_pool(name="soft", bufs=3) as soft,
+        tc.psum_pool(name="acc_pool", bufs=2) as acc_pool,
+        tc.psum_pool(name="score_pool", bufs=2) as score_pool,
+        tc.psum_pool(name="flip_pool", bufs=2) as flip_pool,
+        tc.psum_pool(name="mix_pool", bufs=2) as mix_pool,
+    ):
+        offsets = held.tile([P, N // 16], U16, name="offsets")
+        nc.sync.dma_start(offsets[:], offs)
+
+        wq_sb = held.tile([P, E_BLOCKS, HEADS * P], BF16, name="wq_sb")
+        wk_sb = held.tile([P, E_BLOCKS, KV_HEADS * P], BF16, name="wk_sb")
+        wv_sb = held.tile([P, E_BLOCKS, KV_HEADS * P], BF16, name="wv_sb")
+        wo_sb = held.tile([P, HEADS, E], BF16, name="wo_sb")
+        for tile, source in ((wq_sb, wq), (wk_sb, wk), (wv_sb, wv), (wo_sb, wo)):
+            nc.scalar.dma_start(tile[:], source.rearrange("(k p) m -> p k m", p=P))
+
+        x_blocks = x.rearrange("(k p) n -> p k n", p=P)
+        x_sb = []
+        for b in range(N_SEQ):
+            x_seq = held.tile([P, E_BLOCKS, SEQ], BF16, name=f"x_seq{b}")
+            nc.sync.dma_start(x_seq[:], x_blocks[:, :, b * SEQ : (b + 1) * SEQ])
+            x_sb.append(x_seq)
+
+        cos = held.tile([P, POSITIONS], F32, name="cos")
+        sin = held.tile([P, POSITIONS], F32, name="sin")
+        nc.gpsimd.dma_start(cos[:], rope[0:P, :])
+        nc.gpsimd.dma_start(sin[:], rope[P : 2 * P, :])
+
+        identity = held.tile([P, P], BF16, name="identity")
+        make_identity(nc, identity[:])
+
+        mask = held.tile([P, 2 * P], BF16, name="mask")
+        nc.gpsimd.memset(mask[:], 0.0)
+        nc.gpsimd.affine_select(
+            out=mask[:], in_=mask[:], compare_op=IS_GE, fill=MASKED,
+            base=0, pattern=[[1, 2 * P]], channel_multiplier=-1,
+        )
+        nc.gpsimd.affine_select(
+            out=mask[:], in_=mask[:], compare_op=IS_GE, fill=MASKED,
+            base=P, pattern=[[-1, 2 * P]], channel_multiplier=1,
+        )
+
+        def rotated_weights(weights, columns, name):
+            rotated = held.tile([P, E_BLOCKS, columns], BF16, name=name)
+            halves_in = weights[:].rearrange("p k (g s d) -> p k g s d", s=2, d=HALF)
+            halves_out = rotated[:].rearrange("p k (g s d) -> p k g s d", s=2, d=HALF)
+            nc.vector.tensor_scalar_mul(halves_out[:, :, :, 0, :], halves_in[:, :, :, 1, :], -1.0)
+            nc.vector.tensor_copy(halves_out[:, :, :, 1, :], halves_in[:, :, :, 0, :])
+            return rotated
+
+        wq_rot = rotated_weights(wq_sb, HEADS * P, "wq_rot")
+        wk_rot = rotated_weights(wk_sb, KV_HEADS * P, "wk_rot")
+
+        qr = [held.tile([P, HEADS, SEQ], BF16, name=f"qr{b}") for b in range(N_SEQ)]
+        kr = [held.tile([P, KV_HEADS, SEQ], BF16, name=f"kr{b}") for b in range(N_SEQ)]
+        v_tok = [held.tile([P, BLOCKS, KV_HEADS * P], BF16, name=f"v_tok{b}") for b in range(N_SEQ)]
+        att = [held.tile([P, HEADS, SEQ], BF16, name=f"att{b}") for b in range(N_SEQ)]
+
+        def project(weights, head, b, scale, name):
+            acc = acc_pool.tile([P, SEQ], F32, name="acc")
+            for k in range(E_BLOCKS):
+                nc.tensor.matmul(
+                    acc[:], weights[:, k, head * P : (head + 1) * P], x_sb[b][:, k, :],
+                    start=(k == 0), stop=(k == E_BLOCKS - 1),
+                )
+            projected = work.tile([P, SEQ], F32, name=name)
+            nc.scalar.activation(projected[:], acc[:], COPY, scale=scale)
+            return projected
+
+        def rotary(weights, rotated, head, b, scale, dest):
+            piece = offsets[:, b * SEQ // 16 : (b + 1) * SEQ // 16]
+            a = project(weights, head, b, scale, "a")
+            rot_a = project(rotated, head, b, scale, "rot_a")
+            a_cos = work.tile([P, SEQ], F32, name="a_cos")
+            nc.vector.tensor_tensor(a_cos[:], cos[:].indirect(piece), a[:], MULT)
+            rot_a_sin = work.tile([P, SEQ], F32, name="rot_a_sin")
+            nc.vector.tensor_tensor(rot_a_sin[:], sin[:].indirect(piece), rot_a[:], MULT)
+            nc.gpsimd.tensor_tensor(dest, a_cos[:], rot_a_sin[:], ADD)
+
+        def projections(b):
+            for u in range(KV_HEADS):
+                rotary(wk_sb, wk_rot, u, b, 1.0, kr[b][:, u, :])
+            for h in range(HEADS):
+                rotary(wq_sb, wq_rot, h, b, 1.0 / math.sqrt(P), qr[b][:, h, :])
+            for t in range(BLOCKS):
+                acc_v = acc_pool.tile([P, KV_HEADS * P], F32, name="acc_v", tag="acc")
+                for k in range(E_BLOCKS):
+                    nc.tensor.matmul(
+                        acc_v[:], x_sb[b][:, k, t * P : (t + 1) * P], wv_sb[:, k, :],
+                        start=(k == 0), stop=(k == E_BLOCKS - 1),
+                    )
+                nc.scalar.copy(v_tok[b][:, t, :], acc_v[:])
+
+        def attention(b, u, block):
+            first_strip = 1 if block == 0 else 0
+            lo = first_strip * P
+            queries = slice(block * P, (block + 1) * P)
+            keys = slice((block - 1) * P + lo, (block + 1) * P)
+
+            scores = score_pool.tile([P, GROUP, 2 * P], F32, name="scores")
+            for g in range(GROUP):
+                nc.tensor.matmul(scores[:, g, lo:], identity[:], mask[:, lo:], start=True, stop=False)
+                nc.tensor.matmul(
+                    scores[:, g, lo:], qr[b][:, GROUP * u + g, queries], kr[b][:, u, keys],
+                    start=False, stop=True,
+                )
+            neg_max = soft.tile([P, GROUP], F32, name="neg_max")
+            nc.vector.tensor_reduce(neg_max[:], scores[:, :, lo:], axis=X_AXIS, op=MAX, negate=True)
+            expd = soft.tile([P, GROUP, 2 * P], F32, name="expd")
+            total = soft.tile([P, GROUP], F32, name="total")
+            for g in range(GROUP):
+                nc.scalar.activation(
+                    expd[:, g, lo:], scores[:, g, lo:], EXP,
+                    bias=neg_max[:, g : g + 1], accum_out=total[:, g : g + 1],
+                )
+            inverse = soft.tile([P, GROUP], F32, name="inverse")
+            nc.vector.reciprocal(inverse[:], total[:])
+            prob = soft.tile([P, GROUP, 2 * P], BF16, name="prob")
+            for g in range(GROUP):
+                nc.vector.tensor_scalar_mul(prob[:, g, lo:], expd[:, g, lo:], inverse[:, g : g + 1])
+
+            flipped = flip_pool.tile([P, 2, GROUP, P], BF16, name="flipped")
+            for s in range(first_strip, 2):
+                for g in range(GROUP):
+                    nc.tensor.transpose(flipped[:, s, g, :], prob[:, g, s * P : (s + 1) * P], identity[:])
+            prob_t = soft.tile([P, 2, GROUP, P], BF16, name="prob_t")
+            nc.vector.tensor_copy(prob_t[:, first_strip:, :, :], flipped[:, first_strip:, :, :])
+
+            mixed = mix_pool.tile([P, GROUP, P], F32, name="mixed")
+            for s in range(first_strip, 2):
+                nc.tensor.matmul(
+                    mixed[:], v_tok[b][:, block - 1 + s, u * P : (u + 1) * P], prob_t[:, s, :, :],
+                    start=(s == first_strip), stop=(s == 1),
+                )
+            nc.scalar.copy(att[b][:, GROUP * u : GROUP * (u + 1), queries], mixed[:])
+
+        def output(b):
+            for m in range(E // P):
+                acc_o = acc_pool.tile([P, SEQ], F32, name="acc_o", tag="acc")
+                for h in range(HEADS):
+                    nc.tensor.matmul(
+                        acc_o[:], wo_sb[:, h, m * P : (m + 1) * P], att[b][:, h, :],
+                        start=(h == 0), stop=(h == HEADS - 1),
+                    )
+                y = work.tile([P, SEQ], F32, name="y")
+                nc.scalar.copy(y[:], acc_o[:])
+                nc.sync.dma_start(out[m * P : (m + 1) * P, b * SEQ : (b + 1) * SEQ], y[:])
+
+        projections(0)
+        for b in range(N_SEQ):
+            if b + 1 < N_SEQ:
+                projections(b + 1)
+            for block in range(BLOCKS):
+                for u in range(KV_HEADS):
+                    attention(b, u, block)
+            output(b)

@@ -4,8 +4,9 @@ import concourse.mybir as mybir
 from concourse.masks import make_identity
 
 BF16, F32, U16 = mybir.dt.bfloat16, mybir.dt.float32, mybir.dt.uint16
-ADD, MULT, MAX, IS_GE = (
+ADD, SUBTRACT, MULT, MAX, IS_GE = (
     mybir.AluOpType.add,
+    mybir.AluOpType.subtract,
     mybir.AluOpType.mult,
     mybir.AluOpType.max,
     mybir.AluOpType.is_ge,
@@ -24,18 +25,28 @@ POSITIONS = 1024
 E_BLOCKS = E // P
 BLOCKS = SEQ // P
 HALF = P // 2
+PAIRS = (KV_HEADS + HEADS) // 2
 MASKED = -1e30
+
+UNITS_PER_SEQ = KV_HEADS * BLOCKS
+JOBS_PER_SEQ = 2 * PAIRS + BLOCKS // 2
+LOOKUPS_PER_SEQ = 4 * PAIRS
+UNITS, JOBS, LOOKUPS = N_SEQ * UNITS_PER_SEQ, N_SEQ * JOBS_PER_SEQ, N_SEQ * LOOKUPS_PER_SEQ
+assert JOBS_PER_SEQ == UNITS_PER_SEQ
 
 SEEN_PAIRS = N_SEQ * (P * (P + 1) // 2 + (SEQ - P) * (P + 1))
 FLOPS = 2 * N * E * (HEADS + 2 * KV_HEADS) * P + 2 * N * HEADS * P * E + 4 * HEADS * P * SEEN_PAIRS
+
+LOOKUP_LAG = 3
+UNIT_LAG = LOOKUP_LAG + 8
 
 
 def tile_unpaddedmistralattention_b_kernel(tc, x, wq, wk, wv, wo, rope, offs, out):
     nc = tc.nc
     with (
         tc.tile_pool(name="held", bufs=1) as held,
-        tc.tile_pool(name="work", bufs=3) as work,
-        tc.tile_pool(name="soft", bufs=3) as soft,
+        tc.tile_pool(name="work", bufs=4) as work,
+        tc.tile_pool(name="soft", bufs=4) as soft,
         tc.psum_pool(name="acc_pool", bufs=2) as acc_pool,
         tc.psum_pool(name="score_pool", bufs=2) as score_pool,
         tc.psum_pool(name="flip_pool", bufs=2) as flip_pool,
@@ -44,24 +55,29 @@ def tile_unpaddedmistralattention_b_kernel(tc, x, wq, wk, wv, wo, rope, offs, ou
         offsets = held.tile([P, N // 16], U16, name="offsets")
         nc.sync.dma_start(offsets[:], offs)
 
-        wq_sb = held.tile([P, E_BLOCKS, HEADS * P], BF16, name="wq_sb")
+        x_blocks = x.rearrange("(k p) n -> p k n", p=P)
+        x_sb = [held.tile([P, E_BLOCKS, SEQ], BF16, name=f"x_seq{b}") for b in range(N_SEQ)]
+        nc.sync.dma_start(x_sb[0][:], x_blocks[:, :, 0:SEQ])
+
         wk_sb = held.tile([P, E_BLOCKS, KV_HEADS * P], BF16, name="wk_sb")
+        wq_sb = held.tile([P, E_BLOCKS, HEADS * P], BF16, name="wq_sb")
+        nc.scalar.dma_start(wk_sb[:], wk.rearrange("(k p) m -> p k m", p=P))
+        nc.scalar.dma_start(wq_sb[:], wq.rearrange("(k p) m -> p k m", p=P))
+
+        cos = [held.tile([P, POSITIONS], F32, name=f"cos{s}") for s in range(2)]
+        sin = [held.tile([P, POSITIONS], F32, name=f"sin{s}") for s in range(2)]
+        for s in range(2):
+            for g in range(2):
+                nc.sync.dma_start(cos[s][g * HALF : (g + 1) * HALF, :], rope[s * HALF : (s + 1) * HALF, :])
+                nc.scalar.dma_start(sin[s][g * HALF : (g + 1) * HALF, :], rope[P + s * HALF : P + (s + 1) * HALF, :])
+
+        for b in range(1, N_SEQ):
+            nc.sync.dma_start(x_sb[b][:], x_blocks[:, :, b * SEQ : (b + 1) * SEQ])
         wv_sb = held.tile([P, E_BLOCKS, KV_HEADS * P], BF16, name="wv_sb")
         wo_sb = held.tile([P, HEADS, E], BF16, name="wo_sb")
-        for tile, source in ((wq_sb, wq), (wk_sb, wk), (wv_sb, wv), (wo_sb, wo)):
-            nc.scalar.dma_start(tile[:], source.rearrange("(k p) m -> p k m", p=P))
-
-        x_blocks = x.rearrange("(k p) n -> p k n", p=P)
-        x_sb = []
-        for b in range(N_SEQ):
-            x_seq = held.tile([P, E_BLOCKS, SEQ], BF16, name=f"x_seq{b}")
-            nc.sync.dma_start(x_seq[:], x_blocks[:, :, b * SEQ : (b + 1) * SEQ])
-            x_sb.append(x_seq)
-
-        cos = held.tile([P, POSITIONS], F32, name="cos")
-        sin = held.tile([P, POSITIONS], F32, name="sin")
-        nc.gpsimd.dma_start(cos[:], rope[0:P, :])
-        nc.gpsimd.dma_start(sin[:], rope[P : 2 * P, :])
+        nc.scalar.dma_start(wv_sb[:], wv.rearrange("(k p) m -> p k m", p=P))
+        nc.scalar.dma_start(wo_sb[:], wo.rearrange("(k p) m -> p k m", p=P))
+        out_blocks = out.rearrange("(m p) n -> p m n", p=P)
 
         identity = held.tile([P, P], BF16, name="identity")
         make_identity(nc, identity[:])
@@ -77,117 +93,167 @@ def tile_unpaddedmistralattention_b_kernel(tc, x, wq, wk, wv, wo, rope, offs, ou
             base=P, pattern=[[-1, 2 * P]], channel_multiplier=1,
         )
 
-        def rotated_weights(weights, columns, name):
-            rotated = held.tile([P, E_BLOCKS, columns], BF16, name=name)
-            halves_in = weights[:].rearrange("p k (g s d) -> p k g s d", s=2, d=HALF)
-            halves_out = rotated[:].rearrange("p k (g s d) -> p k g s d", s=2, d=HALF)
-            nc.vector.tensor_scalar_mul(halves_out[:, :, :, 0, :], halves_in[:, :, :, 1, :], -1.0)
-            nc.vector.tensor_copy(halves_out[:, :, :, 1, :], halves_in[:, :, :, 0, :])
-            return rotated
+        def paired_halves(weights, pairs, name):
+            paired = held.tile([P, E_BLOCKS, pairs, 2, P], BF16, name=name)
+            by_head = weights[:].rearrange("p k (r g s d) -> p k r g s d", g=2, s=2, d=HALF)
+            by_half = paired[:].rearrange("p k r s (g d) -> p k r s g d", g=2)
+            for s in range(2):
+                nc.vector.tensor_copy(by_half[:, :, :, s, :, :], by_head[:, :, :, :, s, :])
+            return paired
 
-        wq_rot = rotated_weights(wq_sb, HEADS * P, "wq_rot")
-        wk_rot = rotated_weights(wk_sb, KV_HEADS * P, "wk_rot")
+        wk_pairs = paired_halves(wk_sb, 1, "wk_pairs")
+        wq_pairs = paired_halves(wq_sb, HEADS // 2, "wq_pairs")
 
-        qr = [held.tile([P, HEADS, SEQ], BF16, name=f"qr{b}") for b in range(N_SEQ)]
-        kr = [held.tile([P, KV_HEADS, SEQ], BF16, name=f"kr{b}") for b in range(N_SEQ)]
+        roped = [held.tile([P, KV_HEADS + HEADS, SEQ], BF16, name=f"roped{b}") for b in range(N_SEQ)]
         v_tok = [held.tile([P, BLOCKS, KV_HEADS * P], BF16, name=f"v_tok{b}") for b in range(N_SEQ)]
         att = [held.tile([P, HEADS, SEQ], BF16, name=f"att{b}") for b in range(N_SEQ)]
 
-        def project(weights, head, b, scale, name):
+        projected = {}
+
+        def projection_job(j):
+            b, part = divmod(j, JOBS_PER_SEQ)
             acc = acc_pool.tile([P, SEQ], F32, name="acc")
-            for k in range(E_BLOCKS):
-                nc.tensor.matmul(
-                    acc[:], weights[:, k, head * P : (head + 1) * P], x_sb[b][:, k, :],
-                    start=(k == 0), stop=(k == E_BLOCKS - 1),
-                )
-            projected = work.tile([P, SEQ], F32, name=name)
-            nc.scalar.activation(projected[:], acc[:], COPY, scale=scale)
-            return projected
-
-        def rotary(weights, rotated, head, b, scale, dest):
-            piece = offsets[:, b * SEQ // 16 : (b + 1) * SEQ // 16]
-            a = project(weights, head, b, scale, "a")
-            rot_a = project(rotated, head, b, scale, "rot_a")
-            a_cos = work.tile([P, SEQ], F32, name="a_cos")
-            nc.vector.tensor_tensor(a_cos[:], cos[:].indirect(piece), a[:], MULT)
-            rot_a_sin = work.tile([P, SEQ], F32, name="rot_a_sin")
-            nc.vector.tensor_tensor(rot_a_sin[:], sin[:].indirect(piece), rot_a[:], MULT)
-            nc.gpsimd.tensor_tensor(dest, a_cos[:], rot_a_sin[:], ADD)
-
-        def projections(b):
-            for u in range(KV_HEADS):
-                rotary(wk_sb, wk_rot, u, b, 1.0, kr[b][:, u, :])
-            for h in range(HEADS):
-                rotary(wq_sb, wq_rot, h, b, 1.0 / math.sqrt(P), qr[b][:, h, :])
-            for t in range(BLOCKS):
-                acc_v = acc_pool.tile([P, KV_HEADS * P], F32, name="acc_v", tag="acc")
+            if part < 2 * PAIRS:
+                pair, s = divmod(part, 2)
+                weights = wk_pairs[:, :, 0, s, :] if pair == 0 else wq_pairs[:, :, pair - 1, s, :]
                 for k in range(E_BLOCKS):
                     nc.tensor.matmul(
-                        acc_v[:], x_sb[b][:, k, t * P : (t + 1) * P], wv_sb[:, k, :],
-                        start=(k == 0), stop=(k == E_BLOCKS - 1),
+                        acc[:], weights[:, k, :], x_sb[b][:, k, :], start=(k == 0), stop=(k == E_BLOCKS - 1)
                     )
-                nc.scalar.copy(v_tok[b][:, t, :], acc_v[:])
+                half_in = work.tile([P, SEQ], F32, name="half_in")
+                nc.scalar.activation(half_in[:], acc[:], COPY, scale=(1.0 if pair == 0 else 1.0 / math.sqrt(P)))
+                projected[(b, pair, s)] = half_in
+            else:
+                first = 2 * (part - 2 * PAIRS)
+                width = KV_HEADS * P
+                for t in range(2):
+                    for k in range(E_BLOCKS):
+                        nc.tensor.matmul(
+                            acc[:, t * width : (t + 1) * width],
+                            x_sb[b][:, k, (first + t) * P : (first + t + 1) * P], wv_sb[:, k, :],
+                            start=(k == 0), stop=(k == E_BLOCKS - 1),
+                        )
+                nc.scalar.copy(v_tok[b][:, first : first + 2, :], acc[:])
 
-        def attention(b, u, block):
+        own_term = {}
+
+        def lookup(i):
+            granule, term = divmod(i, 4)
+            b, pair = divmod(granule, PAIRS)
+            s, partner = divmod(term, 2)
+            piece = offsets[:, b * SEQ // 16 : (b + 1) * SEQ // 16]
+            table = sin[s] if partner else cos[s]
+            product = work.tile([P, SEQ], F32, name="product")
+            nc.vector.tensor_tensor(
+                product[:], table[:].indirect(piece), projected[(b, pair, (s + partner) % 2)][:], MULT
+            )
+            if not partner:
+                own_term[(b, pair, s)] = product
+                return
+            half_out = work.tile([P, SEQ], BF16, name="half_out")
+            nc.gpsimd.tensor_tensor(half_out[:], own_term[(b, pair, s)][:], product[:], SUBTRACT if s == 0 else ADD)
+            for g in range(2):
+                nc.sync.dma_start(
+                    roped[b][s * HALF : (s + 1) * HALF, 2 * pair + g, :], half_out[g * HALF : (g + 1) * HALF, :]
+                )
+
+        def place(n):
+            b, rest = divmod(n, UNITS_PER_SEQ)
+            u, block = divmod(rest, BLOCKS)
             first_strip = 1 if block == 0 else 0
-            lo = first_strip * P
-            queries = slice(block * P, (block + 1) * P)
-            keys = slice((block - 1) * P + lo, (block + 1) * P)
+            return b, u, block, first_strip
 
-            scores = score_pool.tile([P, GROUP, 2 * P], F32, name="scores")
+        scores, neg_max, expd, total, inverse, prob, flipped, prob_t, mixed = {}, {}, {}, {}, {}, {}, {}, {}, {}
+
+        def score(n):
+            b, u, block, first_strip = place(n)
+            lo = first_strip * P
+            scores[n] = score_pool.tile([P, GROUP, 2 * P], F32, name="scores")
             for g in range(GROUP):
-                nc.tensor.matmul(scores[:, g, lo:], identity[:], mask[:, lo:], start=True, stop=False)
+                nc.tensor.matmul(scores[n][:, g, lo:], identity[:], mask[:, lo:], start=True, stop=False)
                 nc.tensor.matmul(
-                    scores[:, g, lo:], qr[b][:, GROUP * u + g, queries], kr[b][:, u, keys],
+                    scores[n][:, g, lo:],
+                    roped[b][:, 2 * (1 + u) + g, block * P : (block + 1) * P],
+                    roped[b][:, u, (block - 1) * P + lo : (block + 1) * P],
                     start=False, stop=True,
                 )
-            neg_max = soft.tile([P, GROUP], F32, name="neg_max")
-            nc.vector.tensor_reduce(neg_max[:], scores[:, :, lo:], axis=X_AXIS, op=MAX, negate=True)
-            expd = soft.tile([P, GROUP, 2 * P], F32, name="expd")
-            total = soft.tile([P, GROUP], F32, name="total")
+
+        def maximum(n):
+            lo = place(n)[3] * P
+            neg_max[n] = soft.tile([P, GROUP], F32, name="neg_max")
+            nc.vector.tensor_reduce(neg_max[n][:], scores[n][:, :, lo:], axis=X_AXIS, op=MAX, negate=True)
+
+        def exponentials(n):
+            lo = place(n)[3] * P
+            expd[n] = soft.tile([P, GROUP, 2 * P], F32, name="expd")
+            total[n] = soft.tile([P, GROUP], F32, name="total")
             for g in range(GROUP):
                 nc.scalar.activation(
-                    expd[:, g, lo:], scores[:, g, lo:], EXP,
-                    bias=neg_max[:, g : g + 1], accum_out=total[:, g : g + 1],
+                    expd[n][:, g, lo:], scores[n][:, g, lo:], EXP,
+                    bias=neg_max[n][:, g : g + 1], accum_out=total[n][:, g : g + 1],
                 )
-            inverse = soft.tile([P, GROUP], F32, name="inverse")
-            nc.vector.reciprocal(inverse[:], total[:])
-            prob = soft.tile([P, GROUP, 2 * P], BF16, name="prob")
-            for g in range(GROUP):
-                nc.vector.tensor_scalar_mul(prob[:, g, lo:], expd[:, g, lo:], inverse[:, g : g + 1])
 
-            flipped = flip_pool.tile([P, 2, GROUP, P], BF16, name="flipped")
+        def normalise(n):
+            lo = place(n)[3] * P
+            inverse[n] = soft.tile([P, GROUP], F32, name="inverse")
+            nc.vector.reciprocal(inverse[n][:], total[n][:])
+            prob[n] = soft.tile([P, GROUP, 2 * P], BF16, name="prob")
+            for g in range(GROUP):
+                nc.scalar.activation(prob[n][:, g, lo:], expd[n][:, g, lo:], COPY, scale=inverse[n][:, g : g + 1])
+
+        def flip(n):
+            first_strip = place(n)[3]
+            flipped[n] = flip_pool.tile([P, 2, GROUP, P], BF16, name="flipped")
             for s in range(first_strip, 2):
                 for g in range(GROUP):
-                    nc.tensor.transpose(flipped[:, s, g, :], prob[:, g, s * P : (s + 1) * P], identity[:])
-            prob_t = soft.tile([P, 2, GROUP, P], BF16, name="prob_t")
-            nc.vector.tensor_copy(prob_t[:, first_strip:, :, :], flipped[:, first_strip:, :, :])
+                    nc.tensor.transpose(flipped[n][:, s, g, :], prob[n][:, g, s * P : (s + 1) * P], identity[:])
+            prob_t[n] = soft.tile([P, 2, GROUP, P], BF16, name="prob_t")
+            nc.vector.tensor_copy(prob_t[n][:, first_strip:, :, :], flipped[n][:, first_strip:, :, :])
 
-            mixed = mix_pool.tile([P, GROUP, P], F32, name="mixed")
+        def mix(n):
+            b, u, block, first_strip = place(n)
+            mixed[n] = mix_pool.tile([P, GROUP, P], F32, name="mixed")
             for s in range(first_strip, 2):
                 nc.tensor.matmul(
-                    mixed[:], v_tok[b][:, block - 1 + s, u * P : (u + 1) * P], prob_t[:, s, :, :],
+                    mixed[n][:], v_tok[b][:, block - 1 + s, u * P : (u + 1) * P], prob_t[n][:, s, :, :],
                     start=(s == first_strip), stop=(s == 1),
                 )
-            nc.scalar.copy(att[b][:, GROUP * u : GROUP * (u + 1), queries], mixed[:])
 
-        def output(b):
-            for m in range(E // P):
-                acc_o = acc_pool.tile([P, SEQ], F32, name="acc_o", tag="acc")
+        def keep_mixed(n):
+            b, u, block, first_strip = place(n)
+            nc.scalar.copy(att[b][:, GROUP * u : GROUP * (u + 1), block * P : (block + 1) * P], mixed[n][:])
+
+        def output(n):
+            b, u, block, first_strip = place(n)
+            if u < KV_HEADS - 1:
+                return
+            acc_o = acc_pool.tile([P, E_BLOCKS, P], F32, name="acc_o", tag="acc")
+            for m in range(E_BLOCKS):
                 for h in range(HEADS):
                     nc.tensor.matmul(
-                        acc_o[:], wo_sb[:, h, m * P : (m + 1) * P], att[b][:, h, :],
+                        acc_o[:, m, :], wo_sb[:, h, m * P : (m + 1) * P], att[b][:, h, block * P : (block + 1) * P],
                         start=(h == 0), stop=(h == HEADS - 1),
                     )
-                y = work.tile([P, SEQ], F32, name="y")
-                nc.scalar.copy(y[:], acc_o[:])
-                nc.sync.dma_start(out[m * P : (m + 1) * P, b * SEQ : (b + 1) * SEQ], y[:])
+            y = work.tile([P, E_BLOCKS, P], F32, name="y")
+            nc.scalar.copy(y[:], acc_o[:])
+            nc.sync.dma_start(out_blocks[:, :, b * SEQ + block * P : b * SEQ + (block + 1) * P], y[:])
 
-        projections(0)
-        for b in range(N_SEQ):
-            if b + 1 < N_SEQ:
-                projections(b + 1)
-            for block in range(BLOCKS):
-                for u in range(KV_HEADS):
-                    attention(b, u, block)
-            output(b)
+        def if_unit(stage, n):
+            if 0 <= n < UNITS:
+                stage(n)
+
+        for tick in range(UNIT_LAG + UNITS + 3):
+            n = tick - UNIT_LAG
+            if_unit(mix, n - 2)
+            if_unit(normalise, n - 1)
+            if_unit(maximum, n)
+            if_unit(exponentials, n)
+            if tick < JOBS:
+                projection_job(tick)
+            k = tick - LOOKUP_LAG
+            for i in range(max(0, LOOKUPS_PER_SEQ * k // UNITS_PER_SEQ), min(LOOKUPS, LOOKUPS_PER_SEQ * (k + 1) // UNITS_PER_SEQ)):
+                lookup(i)
+            if_unit(flip, n - 1)
+            if_unit(keep_mixed, n - 2)
+            if_unit(score, n + 1)
+            if_unit(output, n - 3)

@@ -38,7 +38,7 @@ SEEN_PAIRS = N_SEQ * (P * (P + 1) // 2 + (SEQ - P) * (P + 1))
 FLOPS = 2 * N * E * (HEADS + 2 * KV_HEADS) * P + 2 * N * HEADS * P * E + 4 * HEADS * P * SEEN_PAIRS
 
 LOOKUP_LAG = 3
-UNIT_LAG = LOOKUP_LAG + 8
+UNIT_LAG = LOOKUP_LAG + 9
 
 
 def tile_unpaddedmistralattention_b_kernel(tc, x, wq, wk, wv, wo, rope, offs, out):
@@ -47,10 +47,10 @@ def tile_unpaddedmistralattention_b_kernel(tc, x, wq, wk, wv, wo, rope, offs, ou
         tc.tile_pool(name="held", bufs=1) as held,
         tc.tile_pool(name="work", bufs=4) as work,
         tc.tile_pool(name="soft", bufs=4) as soft,
-        tc.psum_pool(name="acc_pool", bufs=2) as acc_pool,
+        tc.psum_pool(name="acc_pool", bufs=3) as acc_pool,
         tc.psum_pool(name="score_pool", bufs=2) as score_pool,
         tc.psum_pool(name="flip_pool", bufs=2) as flip_pool,
-        tc.psum_pool(name="mix_pool", bufs=2) as mix_pool,
+        tc.psum_pool(name="mix_pool", bufs=1) as mix_pool,
     ):
         offsets = held.tile([P, N // 16], U16, name="offsets")
         nc.sync.dma_start(offsets[:], offs)
@@ -163,7 +163,7 @@ def tile_unpaddedmistralattention_b_kernel(tc, x, wq, wk, wv, wo, rope, offs, ou
             first_strip = 1 if block == 0 else 0
             return b, u, block, first_strip
 
-        scores, neg_max, expd, total, inverse, prob, flipped, prob_t, mixed = {}, {}, {}, {}, {}, {}, {}, {}, {}
+        scores, neg_max, expd, total, inverse, prob, flipped, prob_t, mixed, acc_out = {}, {}, {}, {}, {}, {}, {}, {}, {}, {}
 
         def score(n):
             b, u, block, first_strip = place(n)
@@ -207,6 +207,9 @@ def tile_unpaddedmistralattention_b_kernel(tc, x, wq, wk, wv, wo, rope, offs, ou
             for s in range(first_strip, 2):
                 for g in range(GROUP):
                     nc.tensor.transpose(flipped[n][:, s, g, :], prob[n][:, g, s * P : (s + 1) * P], identity[:])
+
+        def keep_flipped(n):
+            first_strip = place(n)[3]
             prob_t[n] = soft.tile([P, 2, GROUP, P], BF16, name="prob_t")
             nc.vector.tensor_copy(prob_t[n][:, first_strip:, :, :], flipped[n][:, first_strip:, :, :])
 
@@ -223,37 +226,44 @@ def tile_unpaddedmistralattention_b_kernel(tc, x, wq, wk, wv, wo, rope, offs, ou
             b, u, block, first_strip = place(n)
             nc.scalar.copy(att[b][:, GROUP * u : GROUP * (u + 1), block * P : (block + 1) * P], mixed[n][:])
 
-        def output(n):
+        def project_out(n):
             b, u, block, first_strip = place(n)
             if u < KV_HEADS - 1:
                 return
-            acc_o = acc_pool.tile([P, E_BLOCKS, P], F32, name="acc_o", tag="acc")
+            acc_out[n] = acc_pool.tile([P, E_BLOCKS, P], F32, name="acc_out", tag="acc")
             for m in range(E_BLOCKS):
                 for h in range(HEADS):
                     nc.tensor.matmul(
-                        acc_o[:, m, :], wo_sb[:, h, m * P : (m + 1) * P], att[b][:, h, block * P : (block + 1) * P],
+                        acc_out[n][:, m, :], wo_sb[:, h, m * P : (m + 1) * P], att[b][:, h, block * P : (block + 1) * P],
                         start=(h == 0), stop=(h == HEADS - 1),
                     )
+
+        def store_out(n):
+            b, u, block, first_strip = place(n)
+            if u < KV_HEADS - 1:
+                return
             y = work.tile([P, E_BLOCKS, P], F32, name="y")
-            nc.scalar.copy(y[:], acc_o[:])
+            nc.scalar.copy(y[:], acc_out[n][:])
             nc.sync.dma_start(out_blocks[:, :, b * SEQ + block * P : b * SEQ + (block + 1) * P], y[:])
 
         def if_unit(stage, n):
             if 0 <= n < UNITS:
                 stage(n)
 
-        for tick in range(UNIT_LAG + UNITS + 3):
+        for tick in range(UNIT_LAG + UNITS + 5):
             n = tick - UNIT_LAG
+            if_unit(score, n + 1)
             if_unit(mix, n - 2)
             if_unit(normalise, n - 1)
             if_unit(maximum, n)
             if_unit(exponentials, n)
+            if_unit(flip, n - 1)
+            if_unit(keep_mixed, n - 2)
+            if_unit(store_out, n - 4)
             if tick < JOBS:
                 projection_job(tick)
             k = tick - LOOKUP_LAG
             for i in range(max(0, LOOKUPS_PER_SEQ * k // UNITS_PER_SEQ), min(LOOKUPS, LOOKUPS_PER_SEQ * (k + 1) // UNITS_PER_SEQ)):
                 lookup(i)
-            if_unit(flip, n - 1)
-            if_unit(keep_mixed, n - 2)
-            if_unit(score, n + 1)
-            if_unit(output, n - 3)
+            if_unit(keep_flipped, n - 1)
+            if_unit(project_out, n - 3)

@@ -151,7 +151,7 @@ def tile_unpaddedmistralattention_b_kernel(tc, x, wq, wk, wv, wo, rope, offs, ou
                 own_term[(b, pair, s)] = product
                 return
             half_out = work.tile([P, SEQ], BF16, name="half_out")
-            nc.gpsimd.tensor_tensor(half_out[:], own_term[(b, pair, s)][:], product[:], SUBTRACT if s == 0 else ADD)
+            nc.vector.tensor_tensor(half_out[:], own_term[(b, pair, s)][:], product[:], SUBTRACT if s == 0 else ADD)
             for g in range(2):
                 nc.sync.dma_start(
                     roped[b][s * HALF : (s + 1) * HALF, 2 * pair + g, :], half_out[g * HALF : (g + 1) * HALF, :]

@@ -38,7 +38,7 @@ SEEN_PAIRS = N_SEQ * (P * (P + 1) // 2 + (SEQ - P) * (P + 1))
 FLOPS = 2 * N * E * (HEADS + 2 * KV_HEADS) * P + 2 * N * HEADS * P * E + 4 * HEADS * P * SEEN_PAIRS
 
 LOOKUP_LAG = 3
-UNIT_LAG = LOOKUP_LAG + 9
+UNIT_LAG = LOOKUP_LAG + 7
 
 
 def tile_unpaddedmistralattention_b_kernel(tc, x, wq, wk, wv, wo, rope, offs, out):
@@ -109,10 +109,12 @@ def tile_unpaddedmistralattention_b_kernel(tc, x, wq, wk, wv, wo, rope, offs, ou
         att = [held.tile([P, HEADS, SEQ], BF16, name=f"att{b}") for b in range(N_SEQ)]
 
         projected = {}
+        job_acc = {}
 
-        def projection_job(j):
+        def job_matmuls(j):
             b, part = divmod(j, JOBS_PER_SEQ)
             acc = acc_pool.tile([P, SEQ], F32, name="acc")
+            job_acc[j] = acc
             if part < 2 * PAIRS:
                 pair, s = divmod(part, 2)
                 weights = wk_pairs[:, :, 0, s, :] if pair == 0 else wq_pairs[:, :, pair - 1, s, :]
@@ -120,9 +122,6 @@ def tile_unpaddedmistralattention_b_kernel(tc, x, wq, wk, wv, wo, rope, offs, ou
                     nc.tensor.matmul(
                         acc[:], weights[:, k, :], x_sb[b][:, k, :], start=(k == 0), stop=(k == E_BLOCKS - 1)
                     )
-                half_in = work.tile([P, SEQ], F32, name="half_in")
-                nc.scalar.activation(half_in[:], acc[:], COPY, scale=(1.0 if pair == 0 else 1.0 / math.sqrt(P)))
-                projected[(b, pair, s)] = half_in
             else:
                 first = 2 * (part - 2 * PAIRS)
                 width = KV_HEADS * P
@@ -133,6 +132,17 @@ def tile_unpaddedmistralattention_b_kernel(tc, x, wq, wk, wv, wo, rope, offs, ou
                             x_sb[b][:, k, (first + t) * P : (first + t + 1) * P], wv_sb[:, k, :],
                             start=(k == 0), stop=(k == E_BLOCKS - 1),
                         )
+
+        def job_copy(j):
+            b, part = divmod(j, JOBS_PER_SEQ)
+            acc = job_acc[j]
+            if part < 2 * PAIRS:
+                pair, s = divmod(part, 2)
+                half_in = work.tile([P, SEQ], F32, name="half_in")
+                nc.scalar.activation(half_in[:], acc[:], COPY, scale=(1.0 if pair == 0 else 1.0 / math.sqrt(P)))
+                projected[(b, pair, s)] = half_in
+            else:
+                first = 2 * (part - 2 * PAIRS)
                 nc.scalar.copy(v_tok[b][:, first : first + 2, :], acc[:])
 
         own_term = {}
@@ -193,13 +203,16 @@ def tile_unpaddedmistralattention_b_kernel(tc, x, wq, wk, wv, wo, rope, offs, ou
                     bias=neg_max[n][:, g : g + 1], accum_out=total[n][:, g : g + 1],
                 )
 
-        def normalise(n):
+        def normalise(n, on_vector):
             lo = place(n)[3] * P
             inverse[n] = soft.tile([P, GROUP], F32, name="inverse")
             nc.vector.reciprocal(inverse[n][:], total[n][:])
             prob[n] = soft.tile([P, GROUP, 2 * P], BF16, name="prob")
             for g in range(GROUP):
-                nc.scalar.activation(prob[n][:, g, lo:], expd[n][:, g, lo:], COPY, scale=inverse[n][:, g : g + 1])
+                if on_vector:
+                    nc.vector.tensor_scalar(prob[n][:, g, lo:], expd[n][:, g, lo:], inverse[n][:, g : g + 1], None, MULT)
+                else:
+                    nc.scalar.activation(prob[n][:, g, lo:], expd[n][:, g, lo:], COPY, scale=inverse[n][:, g : g + 1])
 
         def flip(n):
             first_strip = place(n)[3]
@@ -208,10 +221,13 @@ def tile_unpaddedmistralattention_b_kernel(tc, x, wq, wk, wv, wo, rope, offs, ou
                 for g in range(GROUP):
                     nc.tensor.transpose(flipped[n][:, s, g, :], prob[n][:, g, s * P : (s + 1) * P], identity[:])
 
-        def keep_flipped(n):
+        def keep_flipped(n, on_vector):
             first_strip = place(n)[3]
             prob_t[n] = soft.tile([P, 2, GROUP, P], BF16, name="prob_t")
-            nc.vector.tensor_copy(prob_t[n][:, first_strip:, :, :], flipped[n][:, first_strip:, :, :])
+            if on_vector:
+                nc.vector.tensor_copy(prob_t[n][:, first_strip:, :, :], flipped[n][:, first_strip:, :, :])
+            else:
+                nc.scalar.copy(prob_t[n][:, first_strip:, :, :], flipped[n][:, first_strip:, :, :])
 
         def mix(n):
             b, u, block, first_strip = place(n)
@@ -246,24 +262,27 @@ def tile_unpaddedmistralattention_b_kernel(tc, x, wq, wk, wv, wo, rope, offs, ou
             nc.scalar.copy(y[:], acc_out[n][:])
             nc.sync.dma_start(out_blocks[:, :, b * SEQ + block * P : b * SEQ + (block + 1) * P], y[:])
 
-        def if_unit(stage, n):
+        def if_unit(stage, n, *where):
             if 0 <= n < UNITS:
-                stage(n)
+                stage(n, *where)
 
-        for tick in range(UNIT_LAG + UNITS + 5):
+        for tick in range(UNIT_LAG + UNITS + 6):
             n = tick - UNIT_LAG
-            if_unit(score, n + 1)
-            if_unit(mix, n - 2)
-            if_unit(normalise, n - 1)
-            if_unit(maximum, n)
-            if_unit(exponentials, n)
-            if_unit(flip, n - 1)
-            if_unit(keep_mixed, n - 2)
-            if_unit(store_out, n - 4)
-            if tick < JOBS:
-                projection_job(tick)
             k = tick - LOOKUP_LAG
+            vector_is_free = LOOKUPS_PER_SEQ * k // UNITS_PER_SEQ >= LOOKUPS
+            if tick < JOBS:
+                job_matmuls(tick)
+            if_unit(keep_mixed, n - 3)
+            if_unit(mix, n - 2)
+            if_unit(store_out, n - 5)
+            if_unit(normalise, n - 1, vector_is_free)
+            if_unit(maximum, n)
+            if_unit(score, n + 1)
+            if_unit(flip, n - 1)
+            if_unit(exponentials, n)
+            if tick < JOBS:
+                job_copy(tick)
+            if_unit(keep_flipped, n - 1, vector_is_free)
             for i in range(max(0, LOOKUPS_PER_SEQ * k // UNITS_PER_SEQ), min(LOOKUPS, LOOKUPS_PER_SEQ * (k + 1) // UNITS_PER_SEQ)):
                 lookup(i)
-            if_unit(keep_flipped, n - 1)
             if_unit(project_out, n - 3)

@@ -25,8 +25,13 @@ POSITIONS = 1024
 E_BLOCKS = E // P
 BLOCKS = SEQ // P
 HALF = P // 2
+WINDOW = 128
+SUB = P // GROUP
+SUBS = P // SUB
+STRIP = SUB + WINDOW
 PAIRS = (KV_HEADS + HEADS) // 2
 MASKED = -1e30
+PROB_TILES = 4
 
 UNITS_PER_SEQ = KV_HEADS * BLOCKS
 JOBS_PER_SEQ = 2 * PAIRS + BLOCKS // 2
@@ -38,7 +43,7 @@ SEEN_PAIRS = N_SEQ * (P * (P + 1) // 2 + (SEQ - P) * (P + 1))
 FLOPS = 2 * N * E * (HEADS + 2 * KV_HEADS) * P + 2 * N * HEADS * P * E + 4 * HEADS * P * SEEN_PAIRS
 
 LOOKUP_LAG = 3
-UNIT_LAG = LOOKUP_LAG + 7
+UNIT_LAG = LOOKUP_LAG + 8
 
 
 def tile_unpaddedmistralattention_b_kernel(tc, x, wq, wk, wv, wo, rope, offs, out):
@@ -67,9 +72,9 @@ def tile_unpaddedmistralattention_b_kernel(tc, x, wq, wk, wv, wo, rope, offs, ou
         cos = [held.tile([P, POSITIONS], F32, name=f"cos{s}") for s in range(2)]
         sin = [held.tile([P, POSITIONS], F32, name=f"sin{s}") for s in range(2)]
         for s in range(2):
-            for g in range(2):
-                nc.sync.dma_start(cos[s][g * HALF : (g + 1) * HALF, :], rope[s * HALF : (s + 1) * HALF, :])
-                nc.scalar.dma_start(sin[s][g * HALF : (g + 1) * HALF, :], rope[P + s * HALF : P + (s + 1) * HALF, :])
+            for table, first_row in ((cos[s], s * HALF), (sin[s], P + s * HALF)):
+                for g in range(2):
+                    nc.sync.dma_start(table[g * HALF : (g + 1) * HALF, :], rope[first_row : first_row + HALF, :])
 
         for b in range(1, N_SEQ):
             nc.sync.dma_start(x_sb[b][:], x_blocks[:, :, b * SEQ : (b + 1) * SEQ])
@@ -82,16 +87,24 @@ def tile_unpaddedmistralattention_b_kernel(tc, x, wq, wk, wv, wo, rope, offs, ou
         identity = held.tile([P, P], BF16, name="identity")
         make_identity(nc, identity[:])
 
-        mask = held.tile([P, 2 * P], BF16, name="mask")
+        mask = held.tile([P, STRIP], BF16, name="mask")
+        first_mask = held.tile([P, SUBS, P], BF16, name="first_mask")
         nc.gpsimd.memset(mask[:], 0.0)
-        nc.gpsimd.affine_select(
-            out=mask[:], in_=mask[:], compare_op=IS_GE, fill=MASKED,
-            base=0, pattern=[[1, 2 * P]], channel_multiplier=-1,
-        )
-        nc.gpsimd.affine_select(
-            out=mask[:], in_=mask[:], compare_op=IS_GE, fill=MASKED,
-            base=P, pattern=[[-1, 2 * P]], channel_multiplier=1,
-        )
+        nc.gpsimd.memset(first_mask[:], 0.0)
+        for g in range(GROUP):
+            rows = slice(g * SUB, (g + 1) * SUB)
+            nc.gpsimd.affine_select(
+                out=mask[rows, :], in_=mask[rows, :], compare_op=IS_GE, fill=MASKED,
+                base=0, pattern=[[1, STRIP]], channel_multiplier=-1,
+            )
+            nc.gpsimd.affine_select(
+                out=mask[rows, :], in_=mask[rows, :], compare_op=IS_GE, fill=MASKED,
+                base=WINDOW, pattern=[[-1, STRIP]], channel_multiplier=1,
+            )
+            nc.gpsimd.affine_select(
+                out=first_mask[rows, :, :], in_=first_mask[rows, :, :], compare_op=IS_GE, fill=MASKED,
+                base=0, pattern=[[SUB, SUBS], [-1, P]], channel_multiplier=1,
+            )
 
         def paired_halves(weights, pairs, name):
             paired = held.tile([P, E_BLOCKS, pairs, 2, P], BF16, name=name)
@@ -104,7 +117,8 @@ def tile_unpaddedmistralattention_b_kernel(tc, x, wq, wk, wv, wo, rope, offs, ou
         wk_pairs = paired_halves(wk_sb, 1, "wk_pairs")
         wq_pairs = paired_halves(wq_sb, HEADS // 2, "wq_pairs")
 
-        roped = [held.tile([P, KV_HEADS + HEADS, SEQ], BF16, name=f"roped{b}") for b in range(N_SEQ)]
+        roped_k = [held.tile([P, KV_HEADS, SEQ], BF16, name=f"roped_k{b}") for b in range(N_SEQ)]
+        roped_q = [held.tile([P, KV_HEADS, SEQ // SUB, GROUP, SUB], BF16, name=f"roped_q{b}") for b in range(N_SEQ)]
         v_tok = [held.tile([P, BLOCKS, KV_HEADS * P], BF16, name=f"v_tok{b}") for b in range(N_SEQ)]
         att = [held.tile([P, HEADS, SEQ], BF16, name=f"att{b}") for b in range(N_SEQ)]
 
@@ -162,10 +176,13 @@ def tile_unpaddedmistralattention_b_kernel(tc, x, wq, wk, wv, wo, rope, offs, ou
                 return
             half_out = work.tile([P, SEQ], BF16, name="half_out")
             nc.vector.tensor_tensor(half_out[:], own_term[(b, pair, s)][:], product[:], SUBTRACT if s == 0 else ADD)
+            rows = slice(s * HALF, (s + 1) * HALF)
             for g in range(2):
-                nc.sync.dma_start(
-                    roped[b][s * HALF : (s + 1) * HALF, 2 * pair + g, :], half_out[g * HALF : (g + 1) * HALF, :]
-                )
+                head = half_out[g * HALF : (g + 1) * HALF, :]
+                if pair == 0:
+                    nc.sync.dma_start(roped_k[b][rows, g, :], head)
+                else:
+                    nc.sync.dma_start(roped_q[b][rows, pair - 1, :, g, :], head.rearrange("p (j q) -> p j q", q=SUB))
 
         def place(n):
             b, rest = divmod(n, UNITS_PER_SEQ)
@@ -173,57 +190,62 @@ def tile_unpaddedmistralattention_b_kernel(tc, x, wq, wk, wv, wo, rope, offs, ou
             first_strip = 1 if block == 0 else 0
             return b, u, block, first_strip
 
-        scores, neg_max, expd, total, inverse, prob, flipped, prob_t, mixed, acc_out = {}, {}, {}, {}, {}, {}, {}, {}, {}, {}
+        def keys_of(n):
+            return P if place(n)[3] else STRIP
+
+        prob_ring = [held.tile([P, SUBS, 2 * P], BF16, name=f"prob{i}") for i in range(PROB_TILES)]
+        for prob_tile in prob_ring:
+            nc.gpsimd.memset(prob_tile[:], 0.0)
+
+        scores, neg_max, expd, total, inverse, flipped, prob_t, mixed, acc_out = {}, {}, {}, {}, {}, {}, {}, {}, {}
 
         def score(n):
             b, u, block, first_strip = place(n)
-            lo = first_strip * P
-            scores[n] = score_pool.tile([P, GROUP, 2 * P], F32, name="scores")
-            for g in range(GROUP):
-                nc.tensor.matmul(scores[n][:, g, lo:], identity[:], mask[:, lo:], start=True, stop=False)
+            scores[n] = score_pool.tile([P, SUBS, STRIP], F32, name="scores")
+            for a in range(SUBS):
+                first_key = 0 if first_strip else (block - 1) * P + a * SUB
+                seen = scores[n][:, a, : keys_of(n)]
+                nc.tensor.matmul(seen, identity[:], first_mask[:, a, :] if first_strip else mask[:], start=True, stop=False)
                 nc.tensor.matmul(
-                    scores[n][:, g, lo:],
-                    roped[b][:, 2 * (1 + u) + g, block * P : (block + 1) * P],
-                    roped[b][:, u, (block - 1) * P + lo : (block + 1) * P],
+                    seen, roped_q[b][:, u, SUBS * block + a, :, :], roped_k[b][:, u, first_key : first_key + keys_of(n)],
                     start=False, stop=True,
                 )
 
         def maximum(n):
-            lo = place(n)[3] * P
-            neg_max[n] = soft.tile([P, GROUP], F32, name="neg_max")
-            nc.vector.tensor_reduce(neg_max[n][:], scores[n][:, :, lo:], axis=X_AXIS, op=MAX, negate=True)
+            neg_max[n] = soft.tile([P, SUBS], F32, name="neg_max")
+            nc.vector.tensor_reduce(neg_max[n][:], scores[n][:, :, : keys_of(n)], axis=X_AXIS, op=MAX, negate=True)
 
         def exponentials(n):
-            lo = place(n)[3] * P
-            expd[n] = soft.tile([P, GROUP, 2 * P], F32, name="expd")
-            total[n] = soft.tile([P, GROUP], F32, name="total")
-            for g in range(GROUP):
+            expd[n] = soft.tile([P, SUBS, STRIP], F32, name="expd")
+            total[n] = soft.tile([P, SUBS], F32, name="total")
+            for a in range(SUBS):
                 nc.scalar.activation(
-                    expd[n][:, g, lo:], scores[n][:, g, lo:], EXP,
-                    bias=neg_max[n][:, g : g + 1], accum_out=total[n][:, g : g + 1],
+                    expd[n][:, a, : keys_of(n)], scores[n][:, a, : keys_of(n)], EXP,
+                    bias=neg_max[n][:, a : a + 1], accum_out=total[n][:, a : a + 1],
                 )
 
         def normalise(n, on_vector):
-            lo = place(n)[3] * P
-            inverse[n] = soft.tile([P, GROUP], F32, name="inverse")
+            first_strip = place(n)[3]
+            inverse[n] = soft.tile([P, SUBS], F32, name="inverse")
             nc.vector.reciprocal(inverse[n][:], total[n][:])
-            prob[n] = soft.tile([P, GROUP, 2 * P], BF16, name="prob")
-            for g in range(GROUP):
+            for a in range(SUBS):
+                first_column = P if first_strip else a * SUB
+                weights = prob_ring[n % PROB_TILES][:, a, first_column : first_column + keys_of(n)]
                 if on_vector:
-                    nc.vector.tensor_scalar(prob[n][:, g, lo:], expd[n][:, g, lo:], inverse[n][:, g : g + 1], None, MULT)
+                    nc.vector.tensor_scalar(weights, expd[n][:, a, : keys_of(n)], inverse[n][:, a : a + 1], None, MULT)
                 else:
-                    nc.scalar.activation(prob[n][:, g, lo:], expd[n][:, g, lo:], COPY, scale=inverse[n][:, g : g + 1])
+                    nc.scalar.activation(weights, expd[n][:, a, : keys_of(n)], COPY, scale=inverse[n][:, a : a + 1])
 
         def flip(n):
             first_strip = place(n)[3]
-            flipped[n] = flip_pool.tile([P, 2, GROUP, P], BF16, name="flipped")
+            flipped[n] = flip_pool.tile([P, 2, SUBS, P], BF16, name="flipped")
             for s in range(first_strip, 2):
-                for g in range(GROUP):
-                    nc.tensor.transpose(flipped[n][:, s, g, :], prob[n][:, g, s * P : (s + 1) * P], identity[:])
+                for a in range(SUBS):
+                    nc.tensor.transpose(flipped[n][:, s, a, :], prob_ring[n % PROB_TILES][:, a, s * P : (s + 1) * P], identity[:])
 
         def keep_flipped(n, on_vector):
             first_strip = place(n)[3]
-            prob_t[n] = soft.tile([P, 2, GROUP, P], BF16, name="prob_t")
+            prob_t[n] = soft.tile([P, 2, SUBS, P], BF16, name="prob_t")
             if on_vector:
                 nc.vector.tensor_copy(prob_t[n][:, first_strip:, :, :], flipped[n][:, first_strip:, :, :])
             else:
@@ -231,7 +253,7 @@ def tile_unpaddedmistralattention_b_kernel(tc, x, wq, wk, wv, wo, rope, offs, ou
 
         def mix(n):
             b, u, block, first_strip = place(n)
-            mixed[n] = mix_pool.tile([P, GROUP, P], F32, name="mixed")
+            mixed[n] = mix_pool.tile([P, SUBS, P], F32, name="mixed")
             for s in range(first_strip, 2):
                 nc.tensor.matmul(
                     mixed[n][:], v_tok[b][:, block - 1 + s, u * P : (u + 1) * P], prob_t[n][:, s, :, :],
@@ -240,7 +262,10 @@ def tile_unpaddedmistralattention_b_kernel(tc, x, wq, wk, wv, wo, rope, offs, ou
 
         def keep_mixed(n):
             b, u, block, first_strip = place(n)
-            nc.scalar.copy(att[b][:, GROUP * u : GROUP * (u + 1), block * P : (block + 1) * P], mixed[n][:])
+            heads = att[b][:, GROUP * u : GROUP * (u + 1), block * P : (block + 1) * P]
+            nc.scalar.copy(
+                heads.rearrange("p g (a q) -> p a g q", a=SUBS), mixed[n][:].rearrange("p a (g q) -> p a g q", g=GROUP)
+            )
 
         def project_out(n):
             b, u, block, first_strip = place(n)

@@ -52,10 +52,7 @@ def tile_unpaddedmistralattention_b_kernel(tc, x, wq, wk, wv, wo, rope, offs, ou
         tc.tile_pool(name="held", bufs=1) as held,
         tc.tile_pool(name="work", bufs=4) as work,
         tc.tile_pool(name="soft", bufs=4) as soft,
-        tc.psum_pool(name="acc_pool", bufs=3) as acc_pool,
-        tc.psum_pool(name="score_pool", bufs=2) as score_pool,
-        tc.psum_pool(name="flip_pool", bufs=2) as flip_pool,
-        tc.psum_pool(name="mix_pool", bufs=1) as mix_pool,
+        tc.psum_pool(name="banks", bufs=8) as banks,
     ):
         offsets = held.tile([P, N // 16], U16, name="offsets")
         nc.sync.dma_start(offsets[:], offs)
@@ -127,7 +124,7 @@ def tile_unpaddedmistralattention_b_kernel(tc, x, wq, wk, wv, wo, rope, offs, ou
 
         def job_matmuls(j):
             b, part = divmod(j, JOBS_PER_SEQ)
-            acc = acc_pool.tile([P, SEQ], F32, name="acc")
+            acc = banks.tile([P, SEQ], F32, name="acc", tag="bank")
             job_acc[j] = acc
             if part < 2 * PAIRS:
                 pair, s = divmod(part, 2)
@@ -167,7 +164,7 @@ def tile_unpaddedmistralattention_b_kernel(tc, x, wq, wk, wv, wo, rope, offs, ou
             s, partner = divmod(term, 2)
             piece = offsets[:, b * SEQ // 16 : (b + 1) * SEQ // 16]
             table = sin[s] if partner else cos[s]
-            product = work.tile([P, SEQ], F32, name="product")
+            product = work.tile([P, SEQ], F32, name="product", tag="vector_ring")
             nc.vector.tensor_tensor(
                 product[:], table[:].indirect(piece), projected[(b, pair, (s + partner) % 2)][:], MULT
             )
@@ -201,7 +198,7 @@ def tile_unpaddedmistralattention_b_kernel(tc, x, wq, wk, wv, wo, rope, offs, ou
 
         def score(n):
             b, u, block, first_strip = place(n)
-            scores[n] = score_pool.tile([P, SUBS, STRIP], F32, name="scores")
+            scores[n] = banks.tile([P, SUBS, STRIP], F32, name="scores", tag="bank")
             for a in range(SUBS):
                 first_key = 0 if first_strip else (block - 1) * P + a * SUB
                 seen = scores[n][:, a, : keys_of(n)]
@@ -212,7 +209,7 @@ def tile_unpaddedmistralattention_b_kernel(tc, x, wq, wk, wv, wo, rope, offs, ou
                 )
 
         def maximum(n):
-            neg_max[n] = soft.tile([P, SUBS], F32, name="neg_max")
+            neg_max[n] = work.tile([P, SUBS], F32, name="neg_max", tag="vector_ring")
             nc.vector.tensor_reduce(neg_max[n][:], scores[n][:, :, : keys_of(n)], axis=X_AXIS, op=MAX, negate=True)
 
         def exponentials(n):
@@ -238,7 +235,7 @@ def tile_unpaddedmistralattention_b_kernel(tc, x, wq, wk, wv, wo, rope, offs, ou
 
         def flip(n):
             first_strip = place(n)[3]
-            flipped[n] = flip_pool.tile([P, 2, SUBS, P], BF16, name="flipped")
+            flipped[n] = banks.tile([P, 2, SUBS, P], BF16, name="flipped", tag="bank")
             for s in range(first_strip, 2):
                 for a in range(SUBS):
                     nc.tensor.transpose(flipped[n][:, s, a, :], prob_ring[n % PROB_TILES][:, a, s * P : (s + 1) * P], identity[:])
@@ -253,7 +250,7 @@ def tile_unpaddedmistralattention_b_kernel(tc, x, wq, wk, wv, wo, rope, offs, ou
 
         def mix(n):
             b, u, block, first_strip = place(n)
-            mixed[n] = mix_pool.tile([P, SUBS, P], F32, name="mixed")
+            mixed[n] = banks.tile([P, SUBS, P], F32, name="mixed", tag="bank")
             for s in range(first_strip, 2):
                 nc.tensor.matmul(
                     mixed[n][:], v_tok[b][:, block - 1 + s, u * P : (u + 1) * P], prob_t[n][:, s, :, :],
@@ -271,7 +268,7 @@ def tile_unpaddedmistralattention_b_kernel(tc, x, wq, wk, wv, wo, rope, offs, ou
             b, u, block, first_strip = place(n)
             if u < KV_HEADS - 1:
                 return
-            acc_out[n] = acc_pool.tile([P, E_BLOCKS, P], F32, name="acc_out", tag="acc")
+            acc_out[n] = banks.tile([P, E_BLOCKS, P], F32, name="acc_out", tag="bank")
             for m in range(E_BLOCKS):
                 for h in range(HEADS):
                     nc.tensor.matmul(
@@ -291,6 +288,13 @@ def tile_unpaddedmistralattention_b_kernel(tc, x, wq, wk, wv, wo, rope, offs, ou
             if 0 <= n < UNITS:
                 stage(n, *where)
 
+        def output_steps(stage, n):
+            for unit in range(n - (BLOCKS - 1), n + 1):
+                if 0 <= unit < UNITS:
+                    b, u, block, first_strip = place(unit)
+                    if unit + (block if b < N_SEQ - 1 else 0) == n:
+                        stage(unit)
+
         for tick in range(UNIT_LAG + UNITS + 6):
             n = tick - UNIT_LAG
             k = tick - LOOKUP_LAG
@@ -299,7 +303,7 @@ def tile_unpaddedmistralattention_b_kernel(tc, x, wq, wk, wv, wo, rope, offs, ou
                 job_matmuls(tick)
             if_unit(keep_mixed, n - 3)
             if_unit(mix, n - 2)
-            if_unit(store_out, n - 5)
+            output_steps(store_out, n - 5)
             if_unit(normalise, n - 1, vector_is_free)
             if_unit(maximum, n)
             if_unit(score, n + 1)
@@ -310,4 +314,4 @@ def tile_unpaddedmistralattention_b_kernel(tc, x, wq, wk, wv, wo, rope, offs, ou
             if_unit(keep_flipped, n - 1, vector_is_free)
             for i in range(max(0, LOOKUPS_PER_SEQ * k // UNITS_PER_SEQ), min(LOOKUPS, LOOKUPS_PER_SEQ * (k + 1) // UNITS_PER_SEQ)):
                 lookup(i)
-            if_unit(project_out, n - 3)
+            output_steps(project_out, n - 3)

@@ -42,6 +42,7 @@ assert JOBS_PER_SEQ == UNITS_PER_SEQ
 SEEN_PAIRS = N_SEQ * (P * (P + 1) // 2 + (SEQ - P) * (P + 1))
 FLOPS = 2 * N * E * (HEADS + 2 * KV_HEADS) * P + 2 * N * HEADS * P * E + 4 * HEADS * P * SEEN_PAIRS
 
+HALVES_AHEAD = 12
 LOOKUP_LAG = 3
 UNIT_LAG = LOOKUP_LAG + 8
 
@@ -51,6 +52,7 @@ def tile_unpaddedmistralattention_b_kernel(tc, x, wq, wk, wv, wo, rope, offs, ou
     with (
         tc.tile_pool(name="held", bufs=1) as held,
         tc.tile_pool(name="work", bufs=4) as work,
+        tc.tile_pool(name="ahead", bufs=HALVES_AHEAD) as ahead,
         tc.tile_pool(name="soft", bufs=4) as soft,
         tc.psum_pool(name="banks", bufs=8) as banks,
     ):
@@ -149,7 +151,7 @@ def tile_unpaddedmistralattention_b_kernel(tc, x, wq, wk, wv, wo, rope, offs, ou
             acc = job_acc[j]
             if part < 2 * PAIRS:
                 pair, s = divmod(part, 2)
-                half_in = work.tile([P, SEQ], F32, name="half_in")
+                half_in = ahead.tile([P, SEQ], F32, name="half_in")
                 nc.scalar.activation(half_in[:], acc[:], COPY, scale=(1.0 if pair == 0 else 1.0 / math.sqrt(P)))
                 projected[(b, pair, s)] = half_in
             else:
@@ -284,6 +286,9 @@ def tile_unpaddedmistralattention_b_kernel(tc, x, wq, wk, wv, wo, rope, offs, ou
             nc.scalar.copy(y[:], acc_out[n][:])
             nc.sync.dma_start(out_blocks[:, :, b * SEQ + block * P : b * SEQ + (block + 1) * P], y[:])
 
+        def jobs_before(tick):
+            return min(JOBS, tick + min(tick, UNIT_LAG - 1))
+
         def if_unit(stage, n, *where):
             if 0 <= n < UNITS:
                 stage(n, *where)
@@ -299,8 +304,9 @@ def tile_unpaddedmistralattention_b_kernel(tc, x, wq, wk, wv, wo, rope, offs, ou
             n = tick - UNIT_LAG
             k = tick - LOOKUP_LAG
             vector_is_free = LOOKUPS_PER_SEQ * k // UNITS_PER_SEQ >= LOOKUPS
-            if tick < JOBS:
-                job_matmuls(tick)
+            jobs_now = range(jobs_before(tick), jobs_before(tick + 1))
+            for j in jobs_now:
+                job_matmuls(j)
             if_unit(keep_mixed, n - 3)
             if_unit(mix, n - 2)
             output_steps(store_out, n - 5)
@@ -309,8 +315,8 @@ def tile_unpaddedmistralattention_b_kernel(tc, x, wq, wk, wv, wo, rope, offs, ou
             if_unit(score, n + 1)
             if_unit(flip, n - 1)
             if_unit(exponentials, n)
-            if tick < JOBS:
-                job_copy(tick)
+            for j in jobs_now:
+                job_copy(j)
             if_unit(keep_flipped, n - 1, vector_is_free)
             for i in range(max(0, LOOKUPS_PER_SEQ * k // UNITS_PER_SEQ), min(LOOKUPS, LOOKUPS_PER_SEQ * (k + 1) // UNITS_PER_SEQ)):
                 lookup(i)

@@ -43,7 +43,7 @@ SEEN_PAIRS = N_SEQ * (P * (P + 1) // 2 + (SEQ - P) * (P + 1))
 FLOPS = 2 * N * E * (HEADS + 2 * KV_HEADS) * P + 2 * N * HEADS * P * E + 4 * HEADS * P * SEEN_PAIRS
 
 HALVES_AHEAD = 12
-LOOKUP_LAG = 3
+LOOKUP_LAG = 1
 UNIT_LAG = LOOKUP_LAG + 8
 
 
@@ -297,7 +297,7 @@ def tile_unpaddedmistralattention_b_kernel(tc, x, wq, wk, wv, wo, rope, offs, ou
             for unit in range(n - (BLOCKS - 1), n + 1):
                 if 0 <= unit < UNITS:
                     b, u, block, first_strip = place(unit)
-                    if unit + (block if b < N_SEQ - 1 else 0) == n:
+                    if unit + (block if b < N_SEQ - 2 else 0) == n:
                         stage(unit)
 
         for tick in range(UNIT_LAG + UNITS + 6):

@@ -308,16 +308,16 @@ def tile_unpaddedmistralattention_b_kernel(tc, x, wq, wk, wv, wo, rope, offs, ou
             for j in jobs_now:
                 job_matmuls(j)
             if_unit(keep_mixed, n - 3)
-            if_unit(mix, n - 2)
-            output_steps(store_out, n - 5)
-            if_unit(normalise, n - 1, vector_is_free)
-            if_unit(maximum, n)
             if_unit(score, n + 1)
+            if_unit(mix, n - 2)
+            if_unit(normalise, n - 1, vector_is_free)
+            output_steps(store_out, n - 5)
+            if_unit(maximum, n)
             if_unit(flip, n - 1)
             if_unit(exponentials, n)
             for j in jobs_now:
                 job_copy(j)
             if_unit(keep_flipped, n - 1, vector_is_free)
+            output_steps(project_out, n - 3)
             for i in range(max(0, LOOKUPS_PER_SEQ * k // UNITS_PER_SEQ), min(LOOKUPS, LOOKUPS_PER_SEQ * (k + 1) // UNITS_PER_SEQ)):
                 lookup(i)
-            output_steps(project_out, n - 3)

@@ -35,8 +35,11 @@ PROB_TILES = 4
 
 UNITS_PER_SEQ = KV_HEADS * BLOCKS
 JOBS_PER_SEQ = 2 * PAIRS + BLOCKS // 2
-LOOKUPS_PER_SEQ = 4 * PAIRS
-UNITS, JOBS, LOOKUPS = N_SEQ * UNITS_PER_SEQ, N_SEQ * JOBS_PER_SEQ, N_SEQ * LOOKUPS_PER_SEQ
+LOOKUPS_PER_PIECE = 4 * PAIRS
+LAST_PIECES = 2
+LOOKUPS_WHOLE = (N_SEQ - 1) * LOOKUPS_PER_PIECE
+UNITS, JOBS, LOOKUPS = N_SEQ * UNITS_PER_SEQ, N_SEQ * JOBS_PER_SEQ, LOOKUPS_WHOLE + LAST_PIECES * LOOKUPS_PER_PIECE
+GATHERED = LOOKUPS_PER_PIECE * N
 assert JOBS_PER_SEQ == UNITS_PER_SEQ
 
 SEEN_PAIRS = N_SEQ * (P * (P + 1) // 2 + (SEQ - P) * (P + 1))
@@ -45,6 +48,9 @@ FLOPS = 2 * N * E * (HEADS + 2 * KV_HEADS) * P + 2 * N * HEADS * P * E + 4 * HEA
 HALVES_AHEAD = 12
 LOOKUP_LAG = 1
 UNIT_LAG = LOOKUP_LAG + 8
+COLUMNS_A_TICK = LOOKUPS_PER_PIECE * SEQ // UNITS_PER_SEQ
+QUICK_FROM = (N_SEQ - 2) * UNITS_PER_SEQ + UNIT_LAG - LOOKUP_LAG
+QUICK_COLUMNS_A_TICK = SEQ
 
 
 def tile_unpaddedmistralattention_b_kernel(tc, x, wq, wk, wv, wo, rope, offs, out):
@@ -58,15 +64,15 @@ def tile_unpaddedmistralattention_b_kernel(tc, x, wq, wk, wv, wo, rope, offs, ou
     ):
         offsets = held.tile([P, N // 16], U16, name="offsets")
         nc.sync.dma_start(offsets[:], offs)
+        wk_sb = held.tile([P, E_BLOCKS, KV_HEADS * P], BF16, name="wk_sb")
+        nc.scalar.dma_start(wk_sb[:], wk.rearrange("(k p) m -> p k m", p=P))
 
         x_blocks = x.rearrange("(k p) n -> p k n", p=P)
         x_sb = [held.tile([P, E_BLOCKS, SEQ], BF16, name=f"x_seq{b}") for b in range(N_SEQ)]
-        nc.sync.dma_start(x_sb[0][:], x_blocks[:, :, 0:SEQ])
-
-        wk_sb = held.tile([P, E_BLOCKS, KV_HEADS * P], BF16, name="wk_sb")
+        for k in range(E_BLOCKS):
+            nc.sync.dma_start(x_sb[0][:, k, :], x_blocks[:, k, 0:SEQ])
         wq_sb = held.tile([P, E_BLOCKS, HEADS * P], BF16, name="wq_sb")
-        nc.scalar.dma_start(wk_sb[:], wk.rearrange("(k p) m -> p k m", p=P))
-        nc.scalar.dma_start(wq_sb[:], wq.rearrange("(k p) m -> p k m", p=P))
+        nc.sync.dma_start(wq_sb[:], wq.rearrange("(k p) m -> p k m", p=P))
 
         cos = [held.tile([P, POSITIONS], F32, name=f"cos{s}") for s in range(2)]
         sin = [held.tile([P, POSITIONS], F32, name=f"sin{s}") for s in range(2)]
@@ -75,12 +81,12 @@ def tile_unpaddedmistralattention_b_kernel(tc, x, wq, wk, wv, wo, rope, offs, ou
                 for g in range(2):
                     nc.sync.dma_start(table[g * HALF : (g + 1) * HALF, :], rope[first_row : first_row + HALF, :])
 
+        wv_sb = held.tile([P, E_BLOCKS, KV_HEADS * P], BF16, name="wv_sb")
+        nc.sync.dma_start(wv_sb[:], wv.rearrange("(k p) m -> p k m", p=P))
         for b in range(1, N_SEQ):
             nc.sync.dma_start(x_sb[b][:], x_blocks[:, :, b * SEQ : (b + 1) * SEQ])
-        wv_sb = held.tile([P, E_BLOCKS, KV_HEADS * P], BF16, name="wv_sb")
         wo_sb = held.tile([P, HEADS, E], BF16, name="wo_sb")
-        nc.scalar.dma_start(wv_sb[:], wv.rearrange("(k p) m -> p k m", p=P))
-        nc.scalar.dma_start(wo_sb[:], wo.rearrange("(k p) m -> p k m", p=P))
+        nc.sync.dma_start(wo_sb[:], wo.rearrange("(k p) m -> p k m", p=P))
         out_blocks = out.rearrange("(m p) n -> p m n", p=P)
 
         identity = held.tile([P, P], BF16, name="identity")
@@ -160,32 +166,48 @@ def tile_unpaddedmistralattention_b_kernel(tc, x, wq, wk, wv, wo, rope, offs, ou
 
         own_term = {}
 
+        def piece_of(i):
+            if i < LOOKUPS_WHOLE:
+                b, rest = divmod(i, LOOKUPS_PER_PIECE)
+                return b, 0, SEQ, rest
+            piece, rest = divmod(i - LOOKUPS_WHOLE, LOOKUPS_PER_PIECE)
+            return N_SEQ - 1, piece * (SEQ // LAST_PIECES), SEQ // LAST_PIECES, rest
+
+        def gathered_through(i):
+            return min(i + 1, LOOKUPS_WHOLE) * SEQ + max(0, i + 1 - LOOKUPS_WHOLE) * (SEQ // LAST_PIECES)
+
         def lookup(i):
-            granule, term = divmod(i, 4)
-            b, pair = divmod(granule, PAIRS)
+            b, first, tokens, rest = piece_of(i)
+            pair, term = divmod(rest, 4)
             s, partner = divmod(term, 2)
-            piece = offsets[:, b * SEQ // 16 : (b + 1) * SEQ // 16]
+            ids = offsets[:, (b * SEQ + first) // 16 : (b * SEQ + first + tokens) // 16]
             table = sin[s] if partner else cos[s]
-            product = work.tile([P, SEQ], F32, name="product", tag="vector_ring")
+            product = work.tile([P, tokens], F32, name="product", tag="vector_ring")
             nc.vector.tensor_tensor(
-                product[:], table[:].indirect(piece), projected[(b, pair, (s + partner) % 2)][:], MULT
+                product[:], table[:].indirect(ids), projected[(b, pair, (s + partner) % 2)][:, first : first + tokens], MULT
             )
             if not partner:
-                own_term[(b, pair, s)] = product
+                own_term[(b, first, pair, s)] = product
                 return
-            half_out = work.tile([P, SEQ], BF16, name="half_out")
-            nc.vector.tensor_tensor(half_out[:], own_term[(b, pair, s)][:], product[:], SUBTRACT if s == 0 else ADD)
+            half_out = work.tile([P, tokens], BF16, name="half_out")
+            nc.vector.tensor_tensor(half_out[:], own_term[(b, first, pair, s)][:], product[:], SUBTRACT if s == 0 else ADD)
             rows = slice(s * HALF, (s + 1) * HALF)
             for g in range(2):
                 head = half_out[g * HALF : (g + 1) * HALF, :]
                 if pair == 0:
-                    nc.sync.dma_start(roped_k[b][rows, g, :], head)
+                    nc.sync.dma_start(roped_k[b][rows, g, first : first + tokens], head)
                 else:
-                    nc.sync.dma_start(roped_q[b][rows, pair - 1, :, g, :], head.rearrange("p (j q) -> p j q", q=SUB))
+                    nc.sync.dma_start(
+                        roped_q[b][rows, pair - 1, first // SUB : (first + tokens) // SUB, g, :],
+                        head.rearrange("p (j q) -> p j q", q=SUB),
+                    )
 
         def place(n):
             b, rest = divmod(n, UNITS_PER_SEQ)
-            u, block = divmod(rest, BLOCKS)
+            pieces = LAST_PIECES if b == N_SEQ - 1 else 1
+            piece, rest = divmod(rest, UNITS_PER_SEQ // pieces)
+            u, block = divmod(rest, BLOCKS // pieces)
+            block += piece * (BLOCKS // pieces)
             first_strip = 1 if block == 0 else 0
             return b, u, block, first_strip
 
@@ -300,24 +322,32 @@ def tile_unpaddedmistralattention_b_kernel(tc, x, wq, wk, wv, wo, rope, offs, ou
                     if unit + (block if b < N_SEQ - 2 else 0) == n:
                         stage(unit)
 
+        def gathered_before(k):
+            return COLUMNS_A_TICK * min(k, QUICK_FROM) + QUICK_COLUMNS_A_TICK * max(0, k - QUICK_FROM)
+
         for tick in range(UNIT_LAG + UNITS + 6):
             n = tick - UNIT_LAG
             k = tick - LOOKUP_LAG
-            vector_is_free = LOOKUPS_PER_SEQ * k // UNITS_PER_SEQ >= LOOKUPS
+            vector_is_free = gathered_before(k) >= GATHERED
             jobs_now = range(jobs_before(tick), jobs_before(tick + 1))
             for j in jobs_now:
                 job_matmuls(j)
+            quick = k >= QUICK_FROM
             if_unit(keep_mixed, n - 3)
-            if_unit(score, n + 1)
+            if not quick:
+                if_unit(score, n + 1)
             if_unit(mix, n - 2)
             if_unit(normalise, n - 1, vector_is_free)
             output_steps(store_out, n - 5)
             if_unit(maximum, n)
             if_unit(flip, n - 1)
+            if quick:
+                if_unit(score, n + 1)
             if_unit(exponentials, n)
             for j in jobs_now:
                 job_copy(j)
             if_unit(keep_flipped, n - 1, vector_is_free)
             output_steps(project_out, n - 3)
-            for i in range(max(0, LOOKUPS_PER_SEQ * k // UNITS_PER_SEQ), min(LOOKUPS, LOOKUPS_PER_SEQ * (k + 1) // UNITS_PER_SEQ)):
-                lookup(i)
+            for i in range(LOOKUPS):
+                if gathered_before(k) < gathered_through(i) <= gathered_before(k + 1):
+                    lookup(i)

@@ -51,6 +51,9 @@ UNIT_LAG = LOOKUP_LAG + 8
 COLUMNS_A_TICK = LOOKUPS_PER_PIECE * SEQ // UNITS_PER_SEQ
 QUICK_FROM = (N_SEQ - 2) * UNITS_PER_SEQ + UNIT_LAG - LOOKUP_LAG
 QUICK_COLUMNS_A_TICK = SEQ
+PAIRED_FROM = (
+    QUICK_FROM + (GATHERED - COLUMNS_A_TICK * QUICK_FROM) // QUICK_COLUMNS_A_TICK - (UNIT_LAG - LOOKUP_LAG)
+)
 
 
 def tile_unpaddedmistralattention_b_kernel(tc, x, wq, wk, wv, wo, rope, offs, out):
@@ -311,21 +314,29 @@ def tile_unpaddedmistralattention_b_kernel(tc, x, wq, wk, wv, wo, rope, offs, ou
         def jobs_before(tick):
             return min(JOBS, tick + min(tick, UNIT_LAG - 1))
 
-        def if_unit(stage, n, *where):
-            if 0 <= n < UNITS:
+        def units_of(slot):
+            if slot < PAIRED_FROM:
+                return [slot] if slot >= 0 else []
+            first = PAIRED_FROM + 2 * (slot - PAIRED_FROM)
+            return [n for n in (first, first + 1) if n < UNITS]
+
+        def slot_of(n):
+            return min(n, PAIRED_FROM) + max(0, n - PAIRED_FROM) // 2
+
+        def each_unit(stage, slot, *where):
+            for n in units_of(slot):
                 stage(n, *where)
 
-        def output_steps(stage, n):
-            for unit in range(n - (BLOCKS - 1), n + 1):
-                if 0 <= unit < UNITS:
-                    b, u, block, first_strip = place(unit)
-                    if unit + (block if b < N_SEQ - 2 else 0) == n:
-                        stage(unit)
+        def output_steps(stage, slot):
+            for unit in range(UNITS):
+                b, u, block, first_strip = place(unit)
+                if slot_of(unit) + (block if b < N_SEQ - 2 else 0) == slot:
+                    stage(unit)
 
         def gathered_before(k):
             return COLUMNS_A_TICK * min(k, QUICK_FROM) + QUICK_COLUMNS_A_TICK * max(0, k - QUICK_FROM)
 
-        for tick in range(UNIT_LAG + UNITS + 6):
+        for tick in range(UNIT_LAG + slot_of(UNITS - 1) + 7):
             n = tick - UNIT_LAG
             k = tick - LOOKUP_LAG
             vector_is_free = gathered_before(k) >= GATHERED
@@ -333,20 +344,20 @@ def tile_unpaddedmistralattention_b_kernel(tc, x, wq, wk, wv, wo, rope, offs, ou
             for j in jobs_now:
                 job_matmuls(j)
             quick = k >= QUICK_FROM
-            if_unit(keep_mixed, n - 3)
+            each_unit(keep_mixed, n - 3)
             if not quick:
-                if_unit(score, n + 1)
-            if_unit(mix, n - 2)
-            if_unit(normalise, n - 1, vector_is_free)
+                each_unit(score, n + 1)
+            each_unit(mix, n - 2)
+            each_unit(normalise, n - 1, vector_is_free)
             output_steps(store_out, n - 5)
-            if_unit(maximum, n)
-            if_unit(flip, n - 1)
+            each_unit(maximum, n)
+            each_unit(flip, n - 1)
             if quick:
-                if_unit(score, n + 1)
-            if_unit(exponentials, n)
+                each_unit(score, n + 1)
+            each_unit(exponentials, n)
             for j in jobs_now:
                 job_copy(j)
-            if_unit(keep_flipped, n - 1, vector_is_free)
+            each_unit(keep_flipped, n - 1, vector_is_free)
             output_steps(project_out, n - 3)
             for i in range(LOOKUPS):
                 if gathered_before(k) < gathered_through(i) <= gathered_before(k + 1):

@@ -37,6 +37,7 @@ UNITS_PER_SEQ = KV_HEADS * BLOCKS
 JOBS_PER_SEQ = 2 * PAIRS + BLOCKS // 2
 LOOKUPS_PER_PIECE = 4 * PAIRS
 LAST_PIECES = 2
+HALF_ORDER = [(pair, s) for s in range(2) for pair in range(2)] + [(PAIRS - 1, s) for s in range(2)]
 LOOKUPS_WHOLE = (N_SEQ - 1) * LOOKUPS_PER_PIECE
 UNITS, JOBS, LOOKUPS = N_SEQ * UNITS_PER_SEQ, N_SEQ * JOBS_PER_SEQ, LOOKUPS_WHOLE + LAST_PIECES * LOOKUPS_PER_PIECE
 GATHERED = LOOKUPS_PER_PIECE * N
@@ -181,8 +182,8 @@ def tile_unpaddedmistralattention_b_kernel(tc, x, wq, wk, wv, wo, rope, offs, ou
 
         def lookup(i):
             b, first, tokens, rest = piece_of(i)
-            pair, term = divmod(rest, 4)
-            s, partner = divmod(term, 2)
+            step, partner = divmod(rest, 2)
+            pair, s = HALF_ORDER[step]
             ids = offsets[:, (b * SEQ + first) // 16 : (b * SEQ + first + tokens) // 16]
             table = sin[s] if partner else cos[s]
             product = work.tile([P, tokens], F32, name="product", tag="vector_ring")

@@ -169,6 +169,7 @@ def tile_unpaddedmistralattention_b_kernel(tc, x, wq, wk, wv, wo, rope, offs, ou
                 nc.scalar.copy(v_tok[b][:, first : first + 2, :], acc[:])
 
         own_term = {}
+        partner_term = {}
 
         def piece_of(i):
             if i < LOOKUPS_WHOLE:
@@ -192,9 +193,19 @@ def tile_unpaddedmistralattention_b_kernel(tc, x, wq, wk, wv, wo, rope, offs, ou
             )
             if not partner:
                 own_term[(b, first, pair, s)] = product
+            else:
+                partner_term[(b, first, pair, s)] = product
+
+        def join_products(i):
+            b, first, tokens, rest = piece_of(i)
+            step, partner = divmod(rest, 2)
+            pair, s = HALF_ORDER[step]
+            if not partner:
                 return
             half_out = work.tile([P, tokens], BF16, name="half_out")
-            nc.vector.tensor_tensor(half_out[:], own_term[(b, first, pair, s)][:], product[:], SUBTRACT if s == 0 else ADD)
+            nc.vector.tensor_tensor(
+                half_out[:], own_term[(b, first, pair, s)][:], partner_term[(b, first, pair, s)][:], SUBTRACT if s == 0 else ADD
+            )
             rows = slice(s * HALF, (s + 1) * HALF)
             for g in range(2):
                 head = half_out[g * HALF : (g + 1) * HALF, :]
@@ -363,3 +374,7 @@ def tile_unpaddedmistralattention_b_kernel(tc, x, wq, wk, wv, wo, rope, offs, ou
             for i in range(LOOKUPS):
                 if gathered_before(k) < gathered_through(i) <= gathered_before(k + 1):
                     lookup(i)
+                    if i > 0:
+                        join_products(i - 1)
+                    if i == LOOKUPS - 1:
+                        join_products(i)

import math

import concourse.mybir as mybir
from concourse.masks import make_identity

BF16, F32, U16 = mybir.dt.bfloat16, mybir.dt.float32, mybir.dt.uint16
ADD, SUBTRACT, MULT, MAX, IS_GE = (
    mybir.AluOpType.add,
    mybir.AluOpType.subtract,
    mybir.AluOpType.mult,
    mybir.AluOpType.max,
    mybir.AluOpType.is_ge,
)
EXP, COPY = mybir.ActivationFunctionType.Exp, mybir.ActivationFunctionType.Copy
X_AXIS = mybir.AxisListType.X

P = 128
E = 512
N = 2048
HEADS, KV_HEADS = 4, 2
GROUP = HEADS // KV_HEADS
SEQ = 512
N_SEQ = N // SEQ
POSITIONS = 1024
E_BLOCKS = E // P
BLOCKS = SEQ // P
HALF = P // 2
WINDOW = 128
SUB = P // GROUP
SUBS = P // SUB
STRIP = SUB + WINDOW
PAIRS = (KV_HEADS + HEADS) // 2
MASKED = -1e30
PROB_TILES = 4

UNITS_PER_SEQ = KV_HEADS * BLOCKS
JOBS_PER_SEQ = 2 * PAIRS + BLOCKS // 2
LOOKUPS_PER_PIECE = 4 * PAIRS
LAST_PIECES = 2
HALF_ORDER = [(pair, s) for s in range(2) for pair in range(2)] + [(PAIRS - 1, s) for s in range(2)]
LOOKUPS_WHOLE = (N_SEQ - 1) * LOOKUPS_PER_PIECE
UNITS, JOBS, LOOKUPS = N_SEQ * UNITS_PER_SEQ, N_SEQ * JOBS_PER_SEQ, LOOKUPS_WHOLE + LAST_PIECES * LOOKUPS_PER_PIECE
GATHERED = LOOKUPS_PER_PIECE * N
assert JOBS_PER_SEQ == UNITS_PER_SEQ

SEEN_PAIRS = N_SEQ * (P * (P + 1) // 2 + (SEQ - P) * (P + 1))
FLOPS = 2 * N * E * (HEADS + 2 * KV_HEADS) * P + 2 * N * HEADS * P * E + 4 * HEADS * P * SEEN_PAIRS

HALVES_AHEAD = 12
LOOKUP_LAG = 1
UNIT_LAG = LOOKUP_LAG + 8
COLUMNS_A_TICK = LOOKUPS_PER_PIECE * SEQ // UNITS_PER_SEQ
QUICK_FROM = (N_SEQ - 2) * UNITS_PER_SEQ + UNIT_LAG - LOOKUP_LAG
QUICK_COLUMNS_A_TICK = SEQ
PAIRED_FROM = (
    QUICK_FROM + (GATHERED - COLUMNS_A_TICK * QUICK_FROM) // QUICK_COLUMNS_A_TICK - (UNIT_LAG - LOOKUP_LAG)
)


def tile_unpaddedmistralattention_b_kernel(tc, x, wq, wk, wv, wo, rope, offs, out):
    nc = tc.nc
    with (
        tc.tile_pool(name="held", bufs=1) as held,
        tc.tile_pool(name="work", bufs=4) as work,
        tc.tile_pool(name="ahead", bufs=HALVES_AHEAD) as ahead,
        tc.tile_pool(name="soft", bufs=4) as soft,
        tc.psum_pool(name="banks", bufs=8) as banks,
    ):
        offsets = held.tile([P, N // 16], U16, name="offsets")
        nc.sync.dma_start(offsets[:], offs)
        wk_sb = held.tile([P, E_BLOCKS, KV_HEADS * P], BF16, name="wk_sb")
        nc.scalar.dma_start(wk_sb[:], wk.rearrange("(k p) m -> p k m", p=P))

        x_blocks = x.rearrange("(k p) n -> p k n", p=P)
        x_sb = [held.tile([P, E_BLOCKS, SEQ], BF16, name=f"x_seq{b}") for b in range(N_SEQ)]
        for k in range(E_BLOCKS):
            nc.sync.dma_start(x_sb[0][:, k, :], x_blocks[:, k, 0:SEQ])
        wq_sb = held.tile([P, E_BLOCKS, HEADS * P], BF16, name="wq_sb")
        nc.sync.dma_start(wq_sb[:], wq.rearrange("(k p) m -> p k m", p=P))

        cos = [held.tile([P, POSITIONS], F32, name=f"cos{s}") for s in range(2)]
        sin = [held.tile([P, POSITIONS], F32, name=f"sin{s}") for s in range(2)]
        for s in range(2):
            for table, first_row in ((cos[s], s * HALF), (sin[s], P + s * HALF)):
                for g in range(2):
                    nc.sync.dma_start(table[g * HALF : (g + 1) * HALF, :], rope[first_row : first_row + HALF, :])

        wv_sb = held.tile([P, E_BLOCKS, KV_HEADS * P], BF16, name="wv_sb")
        nc.sync.dma_start(wv_sb[:], wv.rearrange("(k p) m -> p k m", p=P))
        for b in range(1, N_SEQ):
            nc.sync.dma_start(x_sb[b][:], x_blocks[:, :, b * SEQ : (b + 1) * SEQ])
        wo_sb = held.tile([P, HEADS, E], BF16, name="wo_sb")
        nc.sync.dma_start(wo_sb[:], wo.rearrange("(k p) m -> p k m", p=P))
        out_blocks = out.rearrange("(m p) n -> p m n", p=P)

        identity = held.tile([P, P], BF16, name="identity")
        make_identity(nc, identity[:])

        mask = held.tile([P, STRIP], BF16, name="mask")
        first_mask = held.tile([P, SUBS, P], BF16, name="first_mask")
        nc.gpsimd.memset(mask[:], 0.0)
        nc.gpsimd.memset(first_mask[:], 0.0)
        for g in range(GROUP):
            rows = slice(g * SUB, (g + 1) * SUB)
            nc.gpsimd.affine_select(
                out=mask[rows, :], in_=mask[rows, :], compare_op=IS_GE, fill=MASKED,
                base=0, pattern=[[1, STRIP]], channel_multiplier=-1,
            )
            nc.gpsimd.affine_select(
                out=mask[rows, :], in_=mask[rows, :], compare_op=IS_GE, fill=MASKED,
                base=WINDOW, pattern=[[-1, STRIP]], channel_multiplier=1,
            )
            nc.gpsimd.affine_select(
                out=first_mask[rows, :, :], in_=first_mask[rows, :, :], compare_op=IS_GE, fill=MASKED,
                base=0, pattern=[[SUB, SUBS], [-1, P]], channel_multiplier=1,
            )

        def paired_halves(weights, pairs, name):
            paired = held.tile([P, E_BLOCKS, pairs, 2, P], BF16, name=name)
            by_head = weights[:].rearrange("p k (r g s d) -> p k r g s d", g=2, s=2, d=HALF)
            by_half = paired[:].rearrange("p k r s (g d) -> p k r s g d", g=2)
            for s in range(2):
                nc.vector.tensor_copy(by_half[:, :, :, s, :, :], by_head[:, :, :, :, s, :])
            return paired

        wk_pairs = paired_halves(wk_sb, 1, "wk_pairs")
        wq_pairs = paired_halves(wq_sb, HEADS // 2, "wq_pairs")

        roped_k = [held.tile([P, KV_HEADS, SEQ], BF16, name=f"roped_k{b}") for b in range(N_SEQ)]
        roped_q = [held.tile([P, KV_HEADS, SEQ // SUB, GROUP, SUB], BF16, name=f"roped_q{b}") for b in range(N_SEQ)]
        v_tok = [held.tile([P, BLOCKS, KV_HEADS * P], BF16, name=f"v_tok{b}") for b in range(N_SEQ)]
        att = [held.tile([P, HEADS, SEQ], BF16, name=f"att{b}") for b in range(N_SEQ)]

        projected = {}
        job_acc = {}

        def job_matmuls(j):
            b, part = divmod(j, JOBS_PER_SEQ)
            acc = banks.tile([P, SEQ], F32, name="acc", tag="bank")
            job_acc[j] = acc
            if part < 2 * PAIRS:
                pair, s = divmod(part, 2)
                weights = wk_pairs[:, :, 0, s, :] if pair == 0 else wq_pairs[:, :, pair - 1, s, :]
                for k in range(E_BLOCKS):
                    nc.tensor.matmul(
                        acc[:], weights[:, k, :], x_sb[b][:, k, :], start=(k == 0), stop=(k == E_BLOCKS - 1)
                    )
            else:
                first = 2 * (part - 2 * PAIRS)
                width = KV_HEADS * P
                for t in range(2):
                    for k in range(E_BLOCKS):
                        nc.tensor.matmul(
                            acc[:, t * width : (t + 1) * width],
                            x_sb[b][:, k, (first + t) * P : (first + t + 1) * P], wv_sb[:, k, :],
                            start=(k == 0), stop=(k == E_BLOCKS - 1),
                        )

        def job_copy(j):
            b, part = divmod(j, JOBS_PER_SEQ)
            acc = job_acc[j]
            if part < 2 * PAIRS:
                pair, s = divmod(part, 2)
                half_in = ahead.tile([P, SEQ], F32, name="half_in")
                nc.scalar.activation(half_in[:], acc[:], COPY, scale=(1.0 if pair == 0 else 1.0 / math.sqrt(P)))
                projected[(b, pair, s)] = half_in
            else:
                first = 2 * (part - 2 * PAIRS)
                nc.scalar.copy(v_tok[b][:, first : first + 2, :], acc[:])

        own_term = {}
        partner_term = {}

        def piece_of(i):
            if i < LOOKUPS_WHOLE:
                b, rest = divmod(i, LOOKUPS_PER_PIECE)
                return b, 0, SEQ, rest
            piece, rest = divmod(i - LOOKUPS_WHOLE, LOOKUPS_PER_PIECE)
            return N_SEQ - 1, piece * (SEQ // LAST_PIECES), SEQ // LAST_PIECES, rest

        def gathered_through(i):
            return min(i + 1, LOOKUPS_WHOLE) * SEQ + max(0, i + 1 - LOOKUPS_WHOLE) * (SEQ // LAST_PIECES)

        def lookup(i):
            b, first, tokens, rest = piece_of(i)
            step, partner = divmod(rest, 2)
            pair, s = HALF_ORDER[step]
            ids = offsets[:, (b * SEQ + first) // 16 : (b * SEQ + first + tokens) // 16]
            table = sin[s] if partner else cos[s]
            product = work.tile([P, tokens], F32, name="product", tag="vector_ring")
            nc.vector.tensor_tensor(
                product[:], table[:].indirect(ids), projected[(b, pair, (s + partner) % 2)][:, first : first + tokens], MULT
            )
            if not partner:
                own_term[(b, first, pair, s)] = product
            else:
                partner_term[(b, first, pair, s)] = product

        def join_products(i):
            b, first, tokens, rest = piece_of(i)
            step, partner = divmod(rest, 2)
            pair, s = HALF_ORDER[step]
            if not partner:
                return
            half_out = work.tile([P, tokens], BF16, name="half_out")
            nc.vector.tensor_tensor(
                half_out[:], own_term[(b, first, pair, s)][:], partner_term[(b, first, pair, s)][:], SUBTRACT if s == 0 else ADD
            )
            rows = slice(s * HALF, (s + 1) * HALF)
            for g in range(2):
                head = half_out[g * HALF : (g + 1) * HALF, :]
                if pair == 0:
                    nc.sync.dma_start(roped_k[b][rows, g, first : first + tokens], head)
                else:
                    nc.sync.dma_start(
                        roped_q[b][rows, pair - 1, first // SUB : (first + tokens) // SUB, g, :],
                        head.rearrange("p (j q) -> p j q", q=SUB),
                    )

        def place(n):
            b, rest = divmod(n, UNITS_PER_SEQ)
            pieces = LAST_PIECES if b == N_SEQ - 1 else 1
            piece, rest = divmod(rest, UNITS_PER_SEQ // pieces)
            u, block = divmod(rest, BLOCKS // pieces)
            block += piece * (BLOCKS // pieces)
            first_strip = 1 if block == 0 else 0
            return b, u, block, first_strip

        def keys_of(n):
            return P if place(n)[3] else STRIP

        prob_ring = [held.tile([P, SUBS, 2 * P], BF16, name=f"prob{i}") for i in range(PROB_TILES)]
        for prob_tile in prob_ring:
            nc.gpsimd.memset(prob_tile[:], 0.0)

        scores, neg_max, expd, total, inverse, flipped, prob_t, mixed, acc_out = {}, {}, {}, {}, {}, {}, {}, {}, {}

        def score(n):
            b, u, block, first_strip = place(n)
            scores[n] = banks.tile([P, SUBS, STRIP], F32, name="scores", tag="bank")
            for a in range(SUBS):
                first_key = 0 if first_strip else (block - 1) * P + a * SUB
                seen = scores[n][:, a, : keys_of(n)]
                nc.tensor.matmul(seen, identity[:], first_mask[:, a, :] if first_strip else mask[:], start=True, stop=False)
                nc.tensor.matmul(
                    seen, roped_q[b][:, u, SUBS * block + a, :, :], roped_k[b][:, u, first_key : first_key + keys_of(n)],
                    start=False, stop=True,
                )

        def maximum(n):
            neg_max[n] = work.tile([P, SUBS], F32, name="neg_max", tag="vector_ring")
            nc.vector.tensor_reduce(neg_max[n][:], scores[n][:, :, : keys_of(n)], axis=X_AXIS, op=MAX, negate=True)

        def exponentials(n):
            expd[n] = soft.tile([P, SUBS, STRIP], F32, name="expd")
            total[n] = soft.tile([P, SUBS], F32, name="total")
            for a in range(SUBS):
                nc.scalar.activation(
                    expd[n][:, a, : keys_of(n)], scores[n][:, a, : keys_of(n)], EXP,
                    bias=neg_max[n][:, a : a + 1], accum_out=total[n][:, a : a + 1],
                )

        def normalise(n, on_vector):
            first_strip = place(n)[3]
            inverse[n] = soft.tile([P, SUBS], F32, name="inverse")
            nc.vector.reciprocal(inverse[n][:], total[n][:])
            for a in range(SUBS):
                first_column = P if first_strip else a * SUB
                weights = prob_ring[n % PROB_TILES][:, a, first_column : first_column + keys_of(n)]
                if on_vector:
                    nc.vector.tensor_scalar(weights, expd[n][:, a, : keys_of(n)], inverse[n][:, a : a + 1], None, MULT)
                else:
                    nc.scalar.activation(weights, expd[n][:, a, : keys_of(n)], COPY, scale=inverse[n][:, a : a + 1])

        def flip(n):
            first_strip = place(n)[3]
            flipped[n] = banks.tile([P, 2, SUBS, P], BF16, name="flipped", tag="bank")
            for s in range(first_strip, 2):
                for a in range(SUBS):
                    nc.tensor.transpose(flipped[n][:, s, a, :], prob_ring[n % PROB_TILES][:, a, s * P : (s + 1) * P], identity[:])

        def keep_flipped(n, on_vector):
            first_strip = place(n)[3]
            prob_t[n] = soft.tile([P, 2, SUBS, P], BF16, name="prob_t")
            if on_vector:
                nc.vector.tensor_copy(prob_t[n][:, first_strip:, :, :], flipped[n][:, first_strip:, :, :])
            else:
                nc.scalar.copy(prob_t[n][:, first_strip:, :, :], flipped[n][:, first_strip:, :, :])

        def mix(n):
            b, u, block, first_strip = place(n)
            mixed[n] = banks.tile([P, SUBS, P], F32, name="mixed", tag="bank")
            for s in range(first_strip, 2):
                nc.tensor.matmul(
                    mixed[n][:], v_tok[b][:, block - 1 + s, u * P : (u + 1) * P], prob_t[n][:, s, :, :],
                    start=(s == first_strip), stop=(s == 1),
                )

        def keep_mixed(n):
            b, u, block, first_strip = place(n)
            heads = att[b][:, GROUP * u : GROUP * (u + 1), block * P : (block + 1) * P]
            nc.scalar.copy(
                heads.rearrange("p g (a q) -> p a g q", a=SUBS), mixed[n][:].rearrange("p a (g q) -> p a g q", g=GROUP)
            )

        def project_out(n):
            b, u, block, first_strip = place(n)
            if u < KV_HEADS - 1:
                return
            acc_out[n] = banks.tile([P, E_BLOCKS, P], F32, name="acc_out", tag="bank")
            for m in range(E_BLOCKS):
                for h in range(HEADS):
                    nc.tensor.matmul(
                        acc_out[n][:, m, :], wo_sb[:, h, m * P : (m + 1) * P], att[b][:, h, block * P : (block + 1) * P],
                        start=(h == 0), stop=(h == HEADS - 1),
                    )

        def store_out(n):
            b, u, block, first_strip = place(n)
            if u < KV_HEADS - 1:
                return
            y = work.tile([P, E_BLOCKS, P], F32, name="y")
            nc.scalar.copy(y[:], acc_out[n][:])
            nc.sync.dma_start(out_blocks[:, :, b * SEQ + block * P : b * SEQ + (block + 1) * P], y[:])

        def jobs_before(tick):
            return min(JOBS, tick + min(tick, UNIT_LAG - 1))

        def units_of(slot):
            if slot < PAIRED_FROM:
                return [slot] if slot >= 0 else []
            first = PAIRED_FROM + 2 * (slot - PAIRED_FROM)
            return [n for n in (first, first + 1) if n < UNITS]

        def slot_of(n):
            return min(n, PAIRED_FROM) + max(0, n - PAIRED_FROM) // 2

        def each_unit(stage, slot, *where):
            for n in units_of(slot):
                stage(n, *where)

        def output_steps(stage, slot):
            for unit in range(UNITS):
                b, u, block, first_strip = place(unit)
                if slot_of(unit) + (block if b < N_SEQ - 2 else 0) == slot:
                    stage(unit)

        def gathered_before(k):
            return COLUMNS_A_TICK * min(k, QUICK_FROM) + QUICK_COLUMNS_A_TICK * max(0, k - QUICK_FROM)

        for tick in range(UNIT_LAG + slot_of(UNITS - 1) + 7):
            n = tick - UNIT_LAG
            k = tick - LOOKUP_LAG
            vector_is_free = gathered_before(k) >= GATHERED
            jobs_now = range(jobs_before(tick), jobs_before(tick + 1))
            for j in jobs_now:
                job_matmuls(j)
            quick = k >= QUICK_FROM
            each_unit(keep_mixed, n - 3)
            if not quick:
                each_unit(score, n + 1)
            each_unit(mix, n - 2)
            each_unit(normalise, n - 1, vector_is_free)
            output_steps(store_out, n - 5)
            each_unit(maximum, n)
            each_unit(flip, n - 1)
            if quick:
                each_unit(score, n + 1)
            each_unit(exponentials, n)
            for j in jobs_now:
                job_copy(j)
            each_unit(keep_flipped, n - 1, vector_is_free)
            output_steps(project_out, n - 3)
            for i in range(LOOKUPS):
                if gathered_before(k) < gathered_through(i) <= gathered_before(k + 1):
                    lookup(i)
                    if i > 0:
                        join_products(i - 1)
                    if i == LOOKUPS - 1:
                        join_products(i)
